import numpy as np
import ml_dtypes


def mxq(x, axis, fmt="e4m3"):
    dtype, down = {"e4m3": (ml_dtypes.float8_e4m3fn, 7), "e5m2": (ml_dtypes.float8_e5m2, 14)}[fmt]
    v = np.moveaxis(np.asarray(x, np.float32).astype(ml_dtypes.bfloat16).astype(np.float64), axis, -1)
    blocks = v.reshape(v.shape[:-1] + (-1, 32))
    amax = np.abs(blocks).max(-1, keepdims=True)
    byte = np.maximum(np.where(amax > 0, np.frexp(amax)[1] - 1 + 127, 0) - down, 1)
    scale = np.exp2(byte - 127.0)
    codes = (blocks / scale).astype(np.float32).astype(dtype).astype(np.float64)
    return np.moveaxis((codes * scale).reshape(v.shape), -1, axis)


WIDE = False


def mx_kscale(k):
    if not WIDE:
        return np.ones(k)
    levels = np.array([10, -10, 5, -5, 0])
    a = np.random.permutation(np.resize(levels, k // 512 * 4)).reshape(k // 512, 4)
    idx = np.arange(k)
    return np.exp2(a[idx // 512, idx % 128 // 32])


BF16 = ml_dtypes.bfloat16


def bf(x):
    return np.asarray(x, np.float32).astype(BF16)


def f64(x):
    return np.asarray(x).astype(np.float64)


E2M1 = np.array([0.0, 0.5, 1.0, 1.5, 2.0, 3.0, 4.0, 6.0, -0.0, -0.5, -1.0, -1.5, -2.0, -3.0, -4.0, -6.0])


def pack_weight(w, fmt):
    k, n = w.shape
    w = f64(bf(w)).reshape(k // 32, 32, n)
    amax = np.abs(w).max(1)
    if fmt == "e4m3":
        byte = np.frexp(amax)[1] - 1 + 127 - 7
    else:
        mant, ex = np.frexp(amax / 6.0)
        byte = np.where(mant > 0.5, ex, ex - 1) + 127
    byte = np.clip(np.where(amax > 0, byte, 1), 1, 254)
    scaled = (w * np.exp2(127.0 - byte)[:, None, :]).reshape(k, n).astype(np.float32)
    by_word = np.ascontiguousarray(scaled.reshape(k // 512, 128, 4, n).transpose(0, 1, 3, 2))
    if fmt == "e4m3":
        words = by_word.astype(ml_dtypes.float8_e4m3fn).view(np.uint8)
    else:
        c = by_word.astype(ml_dtypes.float4_e2m1fn).view(np.uint8) & 0xF
        words = c[..., 0::2] | (c[..., 1::2] << 4)
    return np.ascontiguousarray(words), np.ascontiguousarray(byte.astype(np.uint8).reshape(k // 512, 16, n))


def unpack_weight(words, scales, fmt):
    g, p, n, _ = words.shape
    if fmt == "e4m3":
        vals = np.ascontiguousarray(words).view(ml_dtypes.float8_e4m3fn).astype(np.float64)
    else:
        nib = np.empty((g, p, n, 4), np.uint8)
        nib[..., 0::2] = words & 0xF
        nib[..., 1::2] = words >> 4
        vals = E2M1[nib]
    vals = vals * np.repeat(np.exp2(scales.astype(np.float64) - 127.0), 8, axis=1)[..., None]
    return vals.transpose(0, 1, 3, 2).reshape(g * 512, n)


B, L, D, DV, BN = 4, 512, 1024, 1024, 256
SV = 2.0 * B / np.sqrt(L)
SB = 2.0 * B / L


def setup_inputs():
    s, u = mx_kscale(D), mx_kscale(D)
    qp_top = bf(np.random.standard_normal((B, BN, D)) * s)
    kp = bf(np.random.standard_normal((B, L, D)) / s)
    v = bf(np.random.standard_normal((B, L, D)) * u)
    Wv = np.random.standard_normal((DV, D)) * SV / np.sqrt(D) / u[None, :]
    Wv_words, Wv_scales = pack_weight(np.ascontiguousarray(Wv.T), "e4m3")
    bv = bf(np.random.standard_normal(DV) * SB)
    return {"qp_top": qp_top,
            "kp": kp,
            "v": v,
            "Wv_words": Wv_words,
            "Wv_scales": Wv_scales,
            "bv": bv}


def reference(qp_top, kp, v, Wv_words, Wv_scales, bv):
    vp = (mxq(f64(v), 2, "e4m3") @ unpack_weight(Wv_words, Wv_scales, "e4m3")) + f64(bv)
    score = (mxq(f64(qp_top), 2, "e4m3") @ mxq(f64(kp), 2, "e4m3").transpose(0, 2, 1)) * (1.0 / np.sqrt(D))
    e = np.exp(score - score.max(0, keepdims=True))
    attn = e / e.sum(0, keepdims=True)
    return mxq(attn, 2, "e4m3") @ mxq(vp, 1, "e4m3")

@@ -1,0 +1,242 @@
+from contextlib import ExitStack
+
+import concourse.mybir as mybir
+from concourse.masks import make_identity
+
+BF16 = mybir.dt.bfloat16
+F32 = mybir.dt.float32
+I32 = mybir.dt.int32
+U32 = mybir.dt.uint32
+U8 = mybir.dt.uint8
+FP8X4 = mybir.dt.float8_e4m3fn_x4
+ACT = mybir.ActivationFunctionType
+ALU = mybir.AluOpType
+
+B, L, D, DV, BN = 4, 512, 1024, 1024, 256
+P = 128
+PACK = 4
+K_PASS = P * PACK
+PASSES = D // K_PASS
+WORDS = K_PASS // 2
+Q_TILES = BN // P
+BANK = 512
+HALVES = DV // BANK
+PSUM_BANKS = 8
+ATTEND_LAG = 2
+
+FLOPS = 2 * B * (L * D * DV + BN * L * D + BN * L * DV)
+
+
+def tile_bottleneck_attention_pa_kernel(tc, qp_top, kp, v, Wv_words, Wv_scales, bv, out):
+    nc = tc.nc
+    with ExitStack() as ctx:
+        ctx.enter_context(tc.manual_schedule())
+        const = ctx.enter_context(tc.tile_pool(name="const", bufs=1))
+        rows_pool = ctx.enter_context(tc.tile_pool(name="rows", bufs=1))
+        group_pool = ctx.enter_context(tc.tile_pool(name="group", bufs=2))
+        code_pool = ctx.enter_context(tc.tile_pool(name="code", bufs=2))
+        keep = ctx.enter_context(tc.tile_pool(name="keep", bufs=1))
+        soft = ctx.enter_context(tc.tile_pool(name="soft", bufs=2))
+        store_pool = ctx.enter_context(tc.tile_pool(name="store", bufs=3))
+        psum = ctx.enter_context(tc.psum_pool(name="psum", bufs=PSUM_BANKS))
+
+        ident = const.tile([P, P], F32)
+        make_identity(nc, ident[:])
+
+        def load_rows(rows, per_partition, name):
+            tile = rows_pool.tile([P, per_partition, D], BF16, name=name)
+            nc.sync.dma_start(out=tile[:], in_=rows.rearrange("(p t) d -> p t d", t=per_partition))
+            return tile
+
+        query_rows = []
+        key_rows = []
+        for b in range(B):
+            query_rows.append(load_rows(qp_top[b], Q_TILES, "q_rows%d" % b))
+            key_rows.append(load_rows(kp[b], PACK, "k_rows%d" % b))
+
+        w_scales = const.tile([P, PASSES, DV], U8, align_bytes=64)
+        nc.vector.memset(w_scales[:].bitcast(I32), 0)
+        for quadrant in range(4):
+            nc.sync.dma_start(
+                out=w_scales[32 * quadrant : 32 * quadrant + 4, :, :].bitcast(I32),
+                in_=Wv_scales[:, 4 * quadrant : 4 * quadrant + 4, :].rearrange("g r n -> r g n").bitcast(I32),
+            )
+        bias = const.tile([P, DV], BF16)
+        nc.sync.dma_start(out=bias[:], in_=bv.partition_broadcast(P))
+        w_words = const.tile([P, PASSES, DV], U32, align_bytes=64)
+        nc.sync.dma_start(
+            out=w_words[:].bitcast(I32),
+            in_=Wv_words.rearrange("g p n t -> p g (n t)").bitcast(I32),
+        )
+        value_rows = [load_rows(v[b], PACK, "v_rows%d" % b) for b in range(B)]
+
+        def turn_rows(rows, as_weight, copy, tag):
+            row_tiles = rows.shape[1]
+            words = rows[:].bitcast(F32)
+            grouped = group_pool.tile([P, PASSES, row_tiles * P, PACK], BF16, tag=tag, align_bytes=64)
+            step = 2 if as_weight else 1
+            for t in range(row_tiles):
+                turned = psum.tile([P, PASSES, 2, P], F32, tag="bank")
+                for g in range(PASSES):
+                    for u in range(2):
+                        first = WORDS * g + (u if as_weight else P * u)
+                        nc.tensor.transpose(
+                            turned[:, g, u, :], words[:, t, first : first + step * (P - 1) + 1 : step], ident[:]
+                        )
+                copy(
+                    out=grouped[:].bitcast(F32)[:, :, P * t : P * (t + 1), :],
+                    in_=turned[:].rearrange("p g u r -> p g r u"),
+                )
+            return grouped
+
+        def quantise_rows(grouped, tag):
+            columns = grouped.shape[2]
+            codes = code_pool.tile([P, PASSES, columns], U32, tag=tag + "_codes", align_bytes=64)
+            scales = code_pool.tile([P, PASSES, columns], U8, tag=tag + "_scales", align_bytes=64)
+            nc.vector.quantize_mx(
+                out=codes[:].rearrange("p g c -> p (g c)").bitcast(FP8X4),
+                scales=scales[:].rearrange("p g c -> p (g c)"),
+                in_=grouped[:].rearrange("p g c f -> p (g c f)"),
+            )
+            return codes, scales
+
+        def multiply_quad(stationary, moving, columns):
+            acc = psum.tile([P, PACK, P], F32, tag="bank")
+            for t in range(PACK):
+                keys = slice(P * t, P * (t + 1))
+                for g in range(PASSES):
+                    nc.tensor.matmul_mx(
+                        out=acc[:, t, :],
+                        lhsT=stationary[0][:, g, keys].bitcast(FP8X4),
+                        lhsT_scale=stationary[1][:, g, keys],
+                        rhs=moving[0][:, g, columns].bitcast(FP8X4),
+                        rhs_scale=moving[1][:, g, columns],
+                        start=(g == 0),
+                        stop=(g == PASSES - 1),
+                    )
+            return acc[:].rearrange("p t c -> p c t")
+
+        score = [keep.tile([P, B, P * PACK], F32, name="score%d" % s) for s in range(Q_TILES)]
+
+        def turn_queries_and_keys(b):
+            return (
+                turn_rows(query_rows[b], False, nc.vector.tensor_copy, "q_grouped"),
+                turn_rows(key_rows[b], False, nc.scalar.copy, "grouped"),
+            )
+
+        def scores(b, q_mx, k_mx):
+            for s in range(Q_TILES):
+                quad = multiply_quad(k_mx, q_mx, slice(P * s, P * (s + 1)))
+                nc.scalar.copy(out=score[s][:, b, :].rearrange("p (i t) -> p i t", t=PACK), in_=quad)
+
+        width = P * PACK
+        over_b = [P, B, width]
+        attn_codes = [keep.tile([P, B, P], U32, name="attn_codes%d" % s, align_bytes=64) for s in range(Q_TILES)]
+        attn_scales = [keep.tile([P, B, P], U8, name="attn_scales%d" % s, align_bytes=64) for s in range(Q_TILES)]
+
+        def exp_of_shifted(s):
+            x = score[s]
+            pair = soft.tile([P, 2, width], F32, tag="pair", bufs=1)
+            nc.vector.tensor_tensor(out=pair[:], in0=x[:, 0:2, :], in1=x[:, 2:4, :], op=ALU.max)
+            top = soft.tile([P, width], F32, tag="one")
+            nc.vector.tensor_tensor(out=top[:], in0=pair[:, 0, :], in1=pair[:, 1, :], op=ALU.max)
+            nc.vector.tensor_tensor(out=x[:], in0=x[:], in1=top[:].unsqueeze(1).to_broadcast(over_b), op=ALU.subtract)
+            nc.scalar.activation(out=x[:], in_=x[:], func=ACT.Exp, scale=1.0 / 32.0)
+
+        def log_of_sum(s):
+            x = score[s]
+            pair = soft.tile([P, 2, width], F32, tag="pair", bufs=1)
+            nc.vector.tensor_tensor(out=pair[:], in0=x[:, 0:2, :], in1=x[:, 2:4, :], op=ALU.add)
+            total = soft.tile([P, width], F32, tag="one")
+            nc.vector.tensor_tensor(out=total[:], in0=pair[:, 0, :], in1=pair[:, 1, :], op=ALU.add)
+            log_total = soft.tile([P, width], F32, tag="log")
+            nc.scalar.activation(out=log_total[:], in_=total[:], func=ACT.Ln)
+            return log_total
+
+        def inverse_of_sum(log_total):
+            inverse = soft.tile([P, width], F32, tag="inverse")
+            nc.scalar.activation(out=inverse[:], in_=log_total[:], func=ACT.Exp, scale=-1.0)
+            return inverse
+
+        def quantise_weights(s, inverse):
+            attn = soft.tile([P, B, width], BF16, align_bytes=64)
+            nc.vector.tensor_tensor(
+                out=attn[:], in0=score[s][:], in1=inverse[:].unsqueeze(1).to_broadcast(over_b), op=ALU.mult
+            )
+            nc.vector.quantize_mx(
+                out=attn_codes[s][:].rearrange("p b i -> p (b i)").bitcast(FP8X4),
+                scales=attn_scales[s][:].rearrange("p b i -> p (b i)"),
+                in_=attn[:].rearrange("p b c -> p (b c)"),
+            )
+
+        vp_codes = [keep.tile([P, DV], U32, name="vp_codes%d" % b, align_bytes=64) for b in range(B)]
+        vp_scales = [keep.tile([P, DV], U8, name="vp_scales%d" % b, align_bytes=64) for b in range(B)]
+
+        def turn_values(b):
+            return turn_rows(value_rows[b], True, nc.scalar.copy, "grouped")
+
+        def project_values(b, h, v_mx):
+            vp_grouped = group_pool.tile([P, BANK, PACK], BF16, tag="vp_grouped", align_bytes=64)
+            for c in range(BANK // P):
+                n_cols = slice(BANK * h + P * c, BANK * h + P * (c + 1))
+                quad = multiply_quad(v_mx, (w_words, w_scales), n_cols)
+                nc.vector.tensor_tensor(
+                    out=vp_grouped[:, P * c : P * (c + 1), :],
+                    in0=quad,
+                    in1=bias[:, n_cols].unsqueeze(2).to_broadcast([P, P, PACK]),
+                    op=ALU.add,
+                )
+            half = slice(BANK * h, BANK * (h + 1))
+            nc.vector.quantize_mx(
+                out=vp_codes[b][:, half].bitcast(FP8X4),
+                scales=vp_scales[b][:, half],
+                in_=vp_grouped[:].rearrange("p n t -> p (n t)"),
+            )
+
+        def attend(b, h, copies):
+            half = slice(BANK * h, BANK * (h + 1))
+            result = store_pool.tile([P, Q_TILES, BANK], F32)
+            for s in range(Q_TILES):
+                acc = psum.tile([P, BANK], F32, tag="bank")
+                nc.tensor.matmul_mx(
+                    out=acc[:],
+                    lhsT=attn_codes[s][:, b, :].bitcast(FP8X4),
+                    lhsT_scale=attn_scales[s][:, b, :],
+                    rhs=vp_codes[b][:, half].bitcast(FP8X4),
+                    rhs_scale=vp_scales[b][:, half],
+                    start=True,
+                    stop=True,
+                )
+                copies[s](out=result[:, s, :], in_=acc[:])
+            nc.sync.dma_start(out=out[b].rearrange("(p s) n -> p s n", s=Q_TILES)[:, :, half], in_=result[:])
+
+        grouped = turn_queries_and_keys(0)
+        for b in range(B):
+            q_mx = quantise_rows(grouped[0], "q")
+            k_mx = quantise_rows(grouped[1], "k")
+            if b + 1 < B:
+                grouped = turn_queries_and_keys(b + 1)
+            scores(b, q_mx, k_mx)
+
+        v_grouped = {0: turn_values(0)}
+        exp_of_shifted(0)
+        v_grouped[1] = turn_values(1)
+        exp_of_shifted(1)
+        v_mx = {0: quantise_rows(v_grouped[0], "v")}
+        logs = [log_of_sum(s) for s in range(Q_TILES)]
+        inverses = [inverse_of_sum(logs[s]) for s in range(Q_TILES)]
+        v_mx[1] = quantise_rows(v_grouped[1], "v")
+
+        both_scalar = (nc.scalar.copy, nc.scalar.copy)
+        halves = [(b, h) for b in range(B) for h in range(HALVES)]
+        for n, (b, h) in enumerate(halves):
+            if h == 0 and 1 <= b < B - 1:
+                v_mx[b + 1] = quantise_rows(turn_values(b + 1), "v")
+            project_values(b, h, v_mx[b])
+            if (b, h) == (0, HALVES - 1):
+                for s in range(Q_TILES):
+                    quantise_weights(s, inverses[s])
+            if n >= ATTEND_LAG:
+                attend(halves[n - ATTEND_LAG][0], halves[n - ATTEND_LAG][1], both_scalar)
+        attend(halves[-2][0], halves[-2][1], both_scalar)
+        attend(halves[-1][0], halves[-1][1], (nc.scalar.copy, nc.vector.tensor_copy))

@@ -22,7 +22,8 @@ Q_TILES = BN // P
 BANK = 512
 HALVES = DV // BANK
 PSUM_BANKS = 8
-ATTEND_LAG = 2
+WEIGHTS_AT = 5
+ATTENDS_PER_HALF = 4
 
 FLOPS = 2 * B * (L * D * DV + BN * L * D + BN * L * DV)
 
@@ -143,12 +144,16 @@ def tile_bottleneck_attention_pa_kernel(tc, qp_top, kp, v, Wv_words, Wv_scales, 
             nc.vector.tensor_tensor(out=x[:], in0=x[:], in1=top[:].unsqueeze(1).to_broadcast(over_b), op=ALU.subtract)
             nc.scalar.activation(out=x[:], in_=x[:], func=ACT.Exp, scale=1.0 / 32.0)
 
-        def log_of_sum(s):
+        def sum_over_batch(s):
             x = score[s]
-            pair = soft.tile([P, 2, width], F32, tag="pair", bufs=1)
-            nc.vector.tensor_tensor(out=pair[:], in0=x[:, 0:2, :], in1=x[:, 2:4, :], op=ALU.add)
+            pair = soft.tile([P, 2, width], F32, tag="pair_sum", bufs=1)
+            for i in range(2):
+                nc.gpsimd.tensor_tensor(out=pair[:, i, :], in0=x[:, i, :], in1=x[:, i + 2, :], op=ALU.add)
             total = soft.tile([P, width], F32, tag="one")
-            nc.vector.tensor_tensor(out=total[:], in0=pair[:, 0, :], in1=pair[:, 1, :], op=ALU.add)
+            nc.gpsimd.tensor_tensor(out=total[:], in0=pair[:, 0, :], in1=pair[:, 1, :], op=ALU.add)
+            return total
+
+        def log_of(total):
             log_total = soft.tile([P, width], F32, tag="log")
             nc.scalar.activation(out=log_total[:], in_=total[:], func=ACT.Ln)
             return log_total
@@ -158,11 +163,13 @@ def tile_bottleneck_attention_pa_kernel(tc, qp_top, kp, v, Wv_words, Wv_scales, 
             nc.scalar.activation(out=inverse[:], in_=log_total[:], func=ACT.Exp, scale=-1.0)
             return inverse
 
-        def quantise_weights(s, inverse):
+        def weights(s, inverse):
             attn = soft.tile([P, B, width], BF16, align_bytes=64)
-            nc.vector.tensor_tensor(
-                out=attn[:], in0=score[s][:], in1=inverse[:].unsqueeze(1).to_broadcast(over_b), op=ALU.mult
-            )
+            for b in range(B):
+                nc.gpsimd.tensor_tensor(out=attn[:, b, :], in0=score[s][:, b, :], in1=inverse[:], op=ALU.mult)
+            return attn
+
+        def quantise_weights(s, attn):
             nc.vector.quantize_mx(
                 out=attn_codes[s][:].rearrange("p b i -> p (b i)").bitcast(FP8X4),
                 scales=attn_scales[s][:].rearrange("p b i -> p (b i)"),
@@ -222,21 +229,33 @@ def tile_bottleneck_attention_pa_kernel(tc, qp_top, kp, v, Wv_words, Wv_scales, 
         exp_of_shifted(0)
         v_grouped[1] = turn_values(1)
         exp_of_shifted(1)
-        v_mx = {0: quantise_rows(v_grouped[0], "v")}
-        logs = [log_of_sum(s) for s in range(Q_TILES)]
-        inverses = [inverse_of_sum(logs[s]) for s in range(Q_TILES)]
-        v_mx[1] = quantise_rows(v_grouped[1], "v")
+        totals = [sum_over_batch(s) for s in range(Q_TILES)]
+        v_mx = {}
+        for b in range(2):
+            v_mx[b] = quantise_rows(v_grouped[b], "v")
+        v_grouped[2] = turn_values(2)
 
         both_scalar = (nc.scalar.copy, nc.scalar.copy)
+        scalar_and_vector = (nc.scalar.copy, nc.vector.tensor_copy)
         halves = [(b, h) for b in range(B) for h in range(HALVES)]
+        attn = []
+        attended = 0
         for n, (b, h) in enumerate(halves):
-            if h == 0 and 1 <= b < B - 1:
-                v_mx[b + 1] = quantise_rows(turn_values(b + 1), "v")
             project_values(b, h, v_mx[b])
-            if (b, h) == (0, HALVES - 1):
+            if n == 0:
+                logs = [log_of(totals[s]) for s in range(Q_TILES)]
+                inverses = [inverse_of_sum(logs[s]) for s in range(Q_TILES)]
+                attn = [weights(s, inverses[s]) for s in range(Q_TILES)]
+            if h == HALVES - 1 and b + 2 < B:
+                v_mx[b + 2] = quantise_rows(v_grouped[b + 2], "v")
+                if b + 3 < B:
+                    v_grouped[b + 3] = turn_values(b + 3)
+            if n > WEIGHTS_AT:
+                projected = n + 1 if n + 1 == len(halves) else n
+                upto = min(attended + ATTENDS_PER_HALF, projected)
+                for i in range(attended, upto):
+                    attend(halves[i][0], halves[i][1], scalar_and_vector if i + 1 == len(halves) else both_scalar)
+                attended = upto
+            if n == WEIGHTS_AT:
                 for s in range(Q_TILES):
-                    quantise_weights(s, inverses[s])
-            if n >= ATTEND_LAG:
-                attend(halves[n - ATTEND_LAG][0], halves[n - ATTEND_LAG][1], both_scalar)
-        attend(halves[-2][0], halves[-2][1], both_scalar)
-        attend(halves[-1][0], halves[-1][1], (nc.scalar.copy, nc.vector.tensor_copy))
+                    quantise_weights(s, attn[s])

@@ -18,12 +18,13 @@ PACK = 4
 K_PASS = P * PACK
 PASSES = D // K_PASS
 WORDS = K_PASS // 2
+PAIR = 2
 Q_TILES = BN // P
 BANK = 512
 HALVES = DV // BANK
+CHUNKS = BANK // P
 PSUM_BANKS = 8
-WEIGHTS_AT = 5
-ATTENDS_PER_HALF = 4
+GROUPED_BUFS = 6
 
 FLOPS = 2 * B * (L * D * DV + BN * L * D + BN * L * DV)
 
@@ -44,9 +45,24 @@ def tile_bottleneck_attention_pa_kernel(tc, qp_top, kp, v, Wv_words, Wv_scales, 
         ident = const.tile([P, P], F32)
         make_identity(nc, ident[:])
 
-        def load_rows(rows, per_partition, name):
-            tile = rows_pool.tile([P, per_partition, D], BF16, name=name)
-            nc.sync.dma_start(out=tile[:], in_=rows.rearrange("(p t) d -> p t d", t=per_partition))
+        bias_row = const.tile([P, DV], BF16)
+        nc.vector.memset(bias_row[:].bitcast(I32), 0)
+        ones = const.tile([P, P], BF16)
+        nc.vector.memset(ones[:], 1.0)
+        bias = const.tile([P, DV], BF16)
+
+        def spread_bias():
+            for h in range(HALVES):
+                half = slice(BANK * h, BANK * (h + 1))
+                spread = psum.tile([P, BANK], F32, tag="bank")
+                nc.tensor.matmul(out=spread[:], lhsT=ones[:], rhs=bias_row[:, half], start=True, stop=True)
+                nc.scalar.copy(out=bias[:, half], in_=spread[:])
+
+        def load_rows(rows, row_tiles, name):
+            tile = rows_pool.tile([P, row_tiles, D], BF16, name=name)
+            by_partition = rows.rearrange("(p t) d -> p t d", t=row_tiles)
+            for first in range(0, row_tiles, PAIR):
+                nc.sync.dma_start(out=tile[:, first : first + PAIR, :], in_=by_partition[:, first : first + PAIR, :])
             return tile
 
         query_rows = []
@@ -55,6 +71,7 @@ def tile_bottleneck_attention_pa_kernel(tc, qp_top, kp, v, Wv_words, Wv_scales, 
             query_rows.append(load_rows(qp_top[b], Q_TILES, "q_rows%d" % b))
             key_rows.append(load_rows(kp[b], PACK, "k_rows%d" % b))
 
+        nc.sync.dma_start(out=bias_row[0:1, :], in_=bv.unsqueeze(0))
         w_scales = const.tile([P, PASSES, DV], U8, align_bytes=64)
         nc.vector.memset(w_scales[:].bitcast(I32), 0)
         for quadrant in range(4):
@@ -62,8 +79,6 @@ def tile_bottleneck_attention_pa_kernel(tc, qp_top, kp, v, Wv_words, Wv_scales, 
                 out=w_scales[32 * quadrant : 32 * quadrant + 4, :, :].bitcast(I32),
                 in_=Wv_scales[:, 4 * quadrant : 4 * quadrant + 4, :].rearrange("g r n -> r g n").bitcast(I32),
             )
-        bias = const.tile([P, DV], BF16)
-        nc.sync.dma_start(out=bias[:], in_=bv.partition_broadcast(P))
         w_words = const.tile([P, PASSES, DV], U32, align_bytes=64)
         nc.sync.dma_start(
             out=w_words[:].bitcast(I32),
@@ -71,18 +86,19 @@ def tile_bottleneck_attention_pa_kernel(tc, qp_top, kp, v, Wv_words, Wv_scales, 
         )
         value_rows = [load_rows(v[b], PACK, "v_rows%d" % b) for b in range(B)]
 
-        def turn_rows(rows, as_weight, copy, tag):
-            row_tiles = rows.shape[1]
+        def turn_pair(rows, first, as_weight, copy):
             words = rows[:].bitcast(F32)
-            grouped = group_pool.tile([P, PASSES, row_tiles * P, PACK], BF16, tag=tag, align_bytes=64)
+            grouped = group_pool.tile([P, PASSES, PAIR * P, PACK], BF16, tag="grouped", bufs=GROUPED_BUFS, align_bytes=64)
             step = 2 if as_weight else 1
-            for t in range(row_tiles):
+            for t in range(PAIR):
                 turned = psum.tile([P, PASSES, 2, P], F32, tag="bank")
                 for g in range(PASSES):
                     for u in range(2):
-                        first = WORDS * g + (u if as_weight else P * u)
+                        start = WORDS * g + (u if as_weight else P * u)
                         nc.tensor.transpose(
-                            turned[:, g, u, :], words[:, t, first : first + step * (P - 1) + 1 : step], ident[:]
+                            turned[:, g, u, :],
+                            words[:, first + t, start : start + step * (P - 1) + 1 : step],
+                            ident[:],
                         )
                 copy(
                     out=grouped[:].bitcast(F32)[:, :, P * t : P * (t + 1), :],
@@ -90,109 +106,125 @@ def tile_bottleneck_attention_pa_kernel(tc, qp_top, kp, v, Wv_words, Wv_scales, 
                 )
             return grouped
 
-        def quantise_rows(grouped, tag):
-            columns = grouped.shape[2]
-            codes = code_pool.tile([P, PASSES, columns], U32, tag=tag + "_codes", align_bytes=64)
-            scales = code_pool.tile([P, PASSES, columns], U8, tag=tag + "_scales", align_bytes=64)
+        def quantise_pair(grouped, codes, scales):
             nc.vector.quantize_mx(
-                out=codes[:].rearrange("p g c -> p (g c)").bitcast(FP8X4),
-                scales=scales[:].rearrange("p g c -> p (g c)"),
+                out=codes.rearrange("p g c -> p (g c)").bitcast(FP8X4),
+                scales=scales.rearrange("p g c -> p (g c)"),
                 in_=grouped[:].rearrange("p g c f -> p (g c f)"),
             )
+
+        def new_codes(pairs, tag):
+            codes = code_pool.tile([P, pairs, PASSES, PAIR * P], U32, tag=tag + "_codes", align_bytes=64)
+            scales = code_pool.tile([P, pairs, PASSES, PAIR * P], U8, tag=tag + "_scales", align_bytes=64)
             return codes, scales
 
-        def multiply_quad(stationary, moving, columns):
+        def multiply_quad(keys_mx, moving_of_pass):
             acc = psum.tile([P, PACK, P], F32, tag="bank")
             for t in range(PACK):
-                keys = slice(P * t, P * (t + 1))
+                rows = slice(P * (t % PAIR), P * (t % PAIR + 1))
                 for g in range(PASSES):
+                    moving = moving_of_pass(g)
                     nc.tensor.matmul_mx(
                         out=acc[:, t, :],
-                        lhsT=stationary[0][:, g, keys].bitcast(FP8X4),
-                        lhsT_scale=stationary[1][:, g, keys],
-                        rhs=moving[0][:, g, columns].bitcast(FP8X4),
-                        rhs_scale=moving[1][:, g, columns],
+                        lhsT=keys_mx[0][:, t // PAIR, g, rows].bitcast(FP8X4),
+                        lhsT_scale=keys_mx[1][:, t // PAIR, g, rows],
+                        rhs=moving[0].bitcast(FP8X4),
+                        rhs_scale=moving[1],
                         start=(g == 0),
                         stop=(g == PASSES - 1),
                     )
             return acc[:].rearrange("p t c -> p c t")
 
-        score = [keep.tile([P, B, P * PACK], F32, name="score%d" % s) for s in range(Q_TILES)]
+        width = P * PACK
+        score = [keep.tile([P, B, width], F32, name="score%d" % s) for s in range(Q_TILES)]
 
         def turn_queries_and_keys(b):
-            return (
-                turn_rows(query_rows[b], False, nc.vector.tensor_copy, "q_grouped"),
-                turn_rows(key_rows[b], False, nc.scalar.copy, "grouped"),
-            )
+            return [turn_pair(query_rows[b], 0, False, nc.vector.tensor_copy)] + [
+                turn_pair(key_rows[b], first, False, nc.scalar.copy) for first in range(0, PACK, PAIR)
+            ]
+
+        def quantise_queries_and_keys(grouped):
+            q_mx = new_codes(1, "q")
+            k_mx = new_codes(PACK // PAIR, "k")
+            quantise_pair(grouped[1], k_mx[0][:, 0], k_mx[1][:, 0])
+            quantise_pair(grouped[0], q_mx[0][:, 0], q_mx[1][:, 0])
+            quantise_pair(grouped[2], k_mx[0][:, 1], k_mx[1][:, 1])
+            return q_mx, k_mx
 
         def scores(b, q_mx, k_mx):
             for s in range(Q_TILES):
-                quad = multiply_quad(k_mx, q_mx, slice(P * s, P * (s + 1)))
+                queries = slice(P * s, P * (s + 1))
+                quad = multiply_quad(k_mx, lambda g: (q_mx[0][:, 0, g, queries], q_mx[1][:, 0, g, queries]))
                 nc.scalar.copy(out=score[s][:, b, :].rearrange("p (i t) -> p i t", t=PACK), in_=quad)
 
-        width = P * PACK
         over_b = [P, B, width]
-        attn_codes = [keep.tile([P, B, P], U32, name="attn_codes%d" % s, align_bytes=64) for s in range(Q_TILES)]
-        attn_scales = [keep.tile([P, B, P], U8, name="attn_scales%d" % s, align_bytes=64) for s in range(Q_TILES)]
+        both = range(Q_TILES)
+        attn_codes = [keep.tile([P, B, P], U32, name="attn_codes%d" % s, align_bytes=64) for s in both]
+        attn_scales = [keep.tile([P, B, P], U8, name="attn_scales%d" % s, align_bytes=64) for s in both]
 
-        def exp_of_shifted(s):
-            x = score[s]
-            pair = soft.tile([P, 2, width], F32, tag="pair", bufs=1)
-            nc.vector.tensor_tensor(out=pair[:], in0=x[:, 0:2, :], in1=x[:, 2:4, :], op=ALU.max)
-            top = soft.tile([P, width], F32, tag="one")
-            nc.vector.tensor_tensor(out=top[:], in0=pair[:, 0, :], in1=pair[:, 1, :], op=ALU.max)
-            nc.vector.tensor_tensor(out=x[:], in0=x[:], in1=top[:].unsqueeze(1).to_broadcast(over_b), op=ALU.subtract)
-            nc.scalar.activation(out=x[:], in_=x[:], func=ACT.Exp, scale=1.0 / 32.0)
+        def combine(x, op, name):
+            pairs = [soft.tile([P, 2, width], F32, name="pair%d" % s, tag="pair") for s in both]
+            for s in both:
+                nc.vector.tensor_tensor(out=pairs[s][:], in0=x[s][:, 0:2, :], in1=x[s][:, 2:4, :], op=op)
+            single = [soft.tile([P, width], F32, name="%s%d" % (name, s), tag="single", bufs=4) for s in both]
+            for s in both:
+                nc.vector.tensor_tensor(out=single[s][:], in0=pairs[s][:, 0, :], in1=pairs[s][:, 1, :], op=op)
+            return single
 
-        def sum_over_batch(s):
-            x = score[s]
-            pair = soft.tile([P, 2, width], F32, tag="pair_sum", bufs=1)
-            for i in range(2):
-                nc.gpsimd.tensor_tensor(out=pair[:, i, :], in0=x[:, i, :], in1=x[:, i + 2, :], op=ALU.add)
-            total = soft.tile([P, width], F32, tag="one")
-            nc.gpsimd.tensor_tensor(out=total[:], in0=pair[:, 0, :], in1=pair[:, 1, :], op=ALU.add)
-            return total
+        def exp_of_shifted():
+            top = combine(score, ALU.max, "top")
+            for s in both:
+                x = score[s]
+                nc.vector.tensor_tensor(
+                    out=x[:], in0=x[:], in1=top[s][:].unsqueeze(1).to_broadcast(over_b), op=ALU.subtract
+                )
+                nc.scalar.activation(out=x[:], in_=x[:], func=ACT.Exp, scale=1.0 / 32.0)
 
-        def log_of(total):
-            log_total = soft.tile([P, width], F32, tag="log")
-            nc.scalar.activation(out=log_total[:], in_=total[:], func=ACT.Ln)
-            return log_total
-
-        def inverse_of_sum(log_total):
-            inverse = soft.tile([P, width], F32, tag="inverse")
-            nc.scalar.activation(out=inverse[:], in_=log_total[:], func=ACT.Exp, scale=-1.0)
+        def inverse_of(total):
+            logs = [soft.tile([P, width], F32, name="log%d" % s, tag="single", bufs=4) for s in both]
+            for s in both:
+                nc.scalar.activation(out=logs[s][:], in_=total[s][:], func=ACT.Ln)
+            inverse = [soft.tile([P, width], F32, name="inverse%d" % s, tag="single", bufs=4) for s in both]
+            for s in both:
+                nc.scalar.activation(out=inverse[s][:], in_=logs[s][:], func=ACT.Exp, scale=-1.0)
             return inverse
 
-        def weights(s, inverse):
-            attn = soft.tile([P, B, width], BF16, align_bytes=64)
-            for b in range(B):
-                nc.gpsimd.tensor_tensor(out=attn[:, b, :], in0=score[s][:, b, :], in1=inverse[:], op=ALU.mult)
-            return attn
-
-        def quantise_weights(s, attn):
-            nc.vector.quantize_mx(
-                out=attn_codes[s][:].rearrange("p b i -> p (b i)").bitcast(FP8X4),
-                scales=attn_scales[s][:].rearrange("p b i -> p (b i)"),
-                in_=attn[:].rearrange("p b c -> p (b c)"),
-            )
+        def weights(inverse):
+            attn = [soft.tile([P, B, width], BF16, name="attn%d" % s, tag="attn", align_bytes=64) for s in both]
+            for s in both:
+                nc.vector.tensor_tensor(
+                    out=attn[s][:], in0=score[s][:], in1=inverse[s][:].unsqueeze(1).to_broadcast(over_b), op=ALU.mult
+                )
+            for s in both:
+                nc.vector.quantize_mx(
+                    out=attn_codes[s][:].rearrange("p b i -> p (b i)").bitcast(FP8X4),
+                    scales=attn_scales[s][:].rearrange("p b i -> p (b i)"),
+                    in_=attn[s][:].rearrange("p b c -> p (b c)"),
+                )
 
         vp_codes = [keep.tile([P, DV], U32, name="vp_codes%d" % b, align_bytes=64) for b in range(B)]
         vp_scales = [keep.tile([P, DV], U8, name="vp_scales%d" % b, align_bytes=64) for b in range(B)]
 
         def turn_values(b):
-            return turn_rows(value_rows[b], True, nc.scalar.copy, "grouped")
+            return [turn_pair(value_rows[b], first, True, nc.scalar.copy) for first in range(0, PACK, PAIR)]
 
-        def project_values(b, h, v_mx):
-            vp_grouped = group_pool.tile([P, BANK, PACK], BF16, tag="vp_grouped", align_bytes=64)
-            for c in range(BANK // P):
-                n_cols = slice(BANK * h + P * c, BANK * h + P * (c + 1))
-                quad = multiply_quad(v_mx, (w_words, w_scales), n_cols)
-                nc.vector.tensor_tensor(
-                    out=vp_grouped[:, P * c : P * (c + 1), :],
-                    in0=quad,
-                    in1=bias[:, n_cols].unsqueeze(2).to_broadcast([P, P, PACK]),
-                    op=ALU.add,
-                )
+        def quantise_values(grouped):
+            v_mx = new_codes(PACK // PAIR, "v")
+            for pair in range(PACK // PAIR):
+                quantise_pair(grouped[pair], v_mx[0][:, pair], v_mx[1][:, pair])
+            return v_mx
+
+        def project_chunk(h, c, v_mx, vp_grouped):
+            features = slice(BANK * h + P * c, BANK * h + P * (c + 1))
+            quad = multiply_quad(v_mx, lambda g: (w_words[:, g, features], w_scales[:, g, features]))
+            nc.vector.tensor_tensor(
+                out=vp_grouped[:, P * c : P * (c + 1), :],
+                in0=quad,
+                in1=bias[:, features].unsqueeze(2).to_broadcast([P, P, PACK]),
+                op=ALU.add,
+            )
+
+        def quantise_projection(b, h, vp_grouped):
             half = slice(BANK * h, BANK * (h + 1))
             nc.vector.quantize_mx(
                 out=vp_codes[b][:, half].bitcast(FP8X4),
@@ -203,7 +235,7 @@ def tile_bottleneck_attention_pa_kernel(tc, qp_top, kp, v, Wv_words, Wv_scales, 
         def attend(b, h, copies):
             half = slice(BANK * h, BANK * (h + 1))
             result = store_pool.tile([P, Q_TILES, BANK], F32)
-            for s in range(Q_TILES):
+            for s in both:
                 acc = psum.tile([P, BANK], F32, tag="bank")
                 nc.tensor.matmul_mx(
                     out=acc[:],
@@ -219,43 +251,41 @@ def tile_bottleneck_attention_pa_kernel(tc, qp_top, kp, v, Wv_words, Wv_scales, 
 
         grouped = turn_queries_and_keys(0)
         for b in range(B):
-            q_mx = quantise_rows(grouped[0], "q")
-            k_mx = quantise_rows(grouped[1], "k")
+            q_mx, k_mx = quantise_queries_and_keys(grouped)
             if b + 1 < B:
                 grouped = turn_queries_and_keys(b + 1)
             scores(b, q_mx, k_mx)
 
-        v_grouped = {0: turn_values(0)}
-        exp_of_shifted(0)
-        v_grouped[1] = turn_values(1)
-        exp_of_shifted(1)
-        totals = [sum_over_batch(s) for s in range(Q_TILES)]
-        v_mx = {}
+        spread_bias()
+        v_grouped = {}
         for b in range(2):
-            v_mx[b] = quantise_rows(v_grouped[b], "v")
+            v_grouped[b] = turn_values(b)
+        exp_of_shifted()
+        v_mx = {0: quantise_values(v_grouped[0])}
+        total = combine(score, ALU.add, "total")
+        inverse = inverse_of(total)
+        v_mx[1] = quantise_values(v_grouped[1])
         v_grouped[2] = turn_values(2)
 
         both_scalar = (nc.scalar.copy, nc.scalar.copy)
         scalar_and_vector = (nc.scalar.copy, nc.vector.tensor_copy)
         halves = [(b, h) for b in range(B) for h in range(HALVES)]
-        attn = []
-        attended = 0
+        vp_grouped = {}
         for n, (b, h) in enumerate(halves):
-            project_values(b, h, v_mx[b])
-            if n == 0:
-                logs = [log_of(totals[s]) for s in range(Q_TILES)]
-                inverses = [inverse_of_sum(logs[s]) for s in range(Q_TILES)]
-                attn = [weights(s, inverses[s]) for s in range(Q_TILES)]
+            vp_grouped[n] = group_pool.tile([P, BANK, PACK], BF16, name="vp_grouped%d" % n, tag="vp_grouped", align_bytes=64)
+            for c in range(CHUNKS):
+                project_chunk(h, c, v_mx[b], vp_grouped[n])
+                if c == 0 and n > 0:
+                    quantise_projection(halves[n - 1][0], halves[n - 1][1], vp_grouped[n - 1])
             if h == HALVES - 1 and b + 2 < B:
-                v_mx[b + 2] = quantise_rows(v_grouped[b + 2], "v")
+                if b == 0:
+                    weights(inverse)
+                v_mx[b + 2] = quantise_values(v_grouped[b + 2])
                 if b + 3 < B:
                     v_grouped[b + 3] = turn_values(b + 3)
-            if n > WEIGHTS_AT:
-                projected = n + 1 if n + 1 == len(halves) else n
-                upto = min(attended + ATTENDS_PER_HALF, projected)
-                for i in range(attended, upto):
-                    attend(halves[i][0], halves[i][1], scalar_and_vector if i + 1 == len(halves) else both_scalar)
-                attended = upto
-            if n == WEIGHTS_AT:
-                for s in range(Q_TILES):
-                    quantise_weights(s, attn[s])
+            if b >= 2:
+                for i in range(2 * (n - 2 * HALVES), 2 * (n - 2 * HALVES) + 2):
+                    if i < n:
+                        attend(halves[i][0], halves[i][1], both_scalar)
+        quantise_projection(B - 1, HALVES - 1, vp_grouped[len(halves) - 1])
+        attend(B - 1, HALVES - 1, scalar_and_vector)

@@ -32,7 +32,6 @@ FLOPS = 2 * B * (L * D * DV + BN * L * D + BN * L * DV)
 def tile_bottleneck_attention_pa_kernel(tc, qp_top, kp, v, Wv_words, Wv_scales, bv, out):
     nc = tc.nc
     with ExitStack() as ctx:
-        ctx.enter_context(tc.manual_schedule())
         const = ctx.enter_context(tc.tile_pool(name="const", bufs=1))
         rows_pool = ctx.enter_context(tc.tile_pool(name="rows", bufs=1))
         group_pool = ctx.enter_context(tc.tile_pool(name="group", bufs=2))
@@ -44,6 +43,9 @@ def tile_bottleneck_attention_pa_kernel(tc, qp_top, kp, v, Wv_words, Wv_scales, 
 
         ident = const.tile([P, P], F32)
         make_identity(nc, ident[:])
+        warm = const.tile([P, 1], F32)
+        nc.vector.memset(warm[:], 0.0)
+        nc.scalar.activation(out=warm[:], in_=warm[:], func=ACT.Exp)
 
         bias_row = const.tile([P, DV], BF16)
         nc.vector.memset(bias_row[:].bitcast(I32), 0)
@@ -162,17 +164,16 @@ def tile_bottleneck_attention_pa_kernel(tc, qp_top, kp, v, Wv_words, Wv_scales, 
         attn_codes = [keep.tile([P, B, P], U32, name="attn_codes%d" % s, align_bytes=64) for s in both]
         attn_scales = [keep.tile([P, B, P], U8, name="attn_scales%d" % s, align_bytes=64) for s in both]
 
-        def combine(x, op, name):
-            pairs = [soft.tile([P, 2, width], F32, name="pair%d" % s, tag="pair") for s in both]
-            for s in both:
-                nc.vector.tensor_tensor(out=pairs[s][:], in0=x[s][:, 0:2, :], in1=x[s][:, 2:4, :], op=op)
-            single = [soft.tile([P, width], F32, name="%s%d" % (name, s), tag="single", bufs=4) for s in both]
-            for s in both:
-                nc.vector.tensor_tensor(out=single[s][:], in0=pairs[s][:, 0, :], in1=pairs[s][:, 1, :], op=op)
-            return single
+        def over_batch(op, name):
+            folded = [soft.tile([P, width], F32, name="%s%d" % (name, s), tag="single", bufs=4) for s in both]
+            for b in range(1, B):
+                for s in both:
+                    so_far = score[s][:, 0, :] if b == 1 else folded[s][:]
+                    nc.vector.tensor_tensor(out=folded[s][:], in0=so_far, in1=score[s][:, b, :], op=op)
+            return folded
 
         def exp_of_shifted():
-            top = combine(score, ALU.max, "top")
+            top = over_batch(ALU.max, "top")
             for s in both:
                 x = score[s]
                 nc.vector.tensor_tensor(
@@ -262,7 +263,7 @@ def tile_bottleneck_attention_pa_kernel(tc, qp_top, kp, v, Wv_words, Wv_scales, 
             v_grouped[b] = turn_values(b)
         exp_of_shifted()
         v_mx = {0: quantise_values(v_grouped[0])}
-        total = combine(score, ALU.add, "total")
+        total = over_batch(ALU.add, "total")
         inverse = inverse_of(total)
         v_mx[1] = quantise_values(v_grouped[1])
         v_grouped[2] = turn_values(2)

@@ -21,8 +21,9 @@ WORDS = K_PASS // 2
 PAIR = 2
 Q_TILES = BN // P
 BANK = 512
-HALVES = DV // BANK
-CHUNKS = BANK // P
+UNIT = BANK // Q_TILES
+UNITS = DV // UNIT
+CHUNKS = UNIT // P
 PSUM_BANKS = 8
 GROUPED_BUFS = 6
 
@@ -38,7 +39,7 @@ def tile_bottleneck_attention_pa_kernel(tc, qp_top, kp, v, Wv_words, Wv_scales, 
         code_pool = ctx.enter_context(tc.tile_pool(name="code", bufs=2))
         keep = ctx.enter_context(tc.tile_pool(name="keep", bufs=1))
         soft = ctx.enter_context(tc.tile_pool(name="soft", bufs=2))
-        store_pool = ctx.enter_context(tc.tile_pool(name="store", bufs=3))
+        store_pool = ctx.enter_context(tc.tile_pool(name="store", bufs=6))
         psum = ctx.enter_context(tc.psum_pool(name="psum", bufs=PSUM_BANKS))
 
         ident = const.tile([P, P], F32)
@@ -54,11 +55,12 @@ def tile_bottleneck_attention_pa_kernel(tc, qp_top, kp, v, Wv_words, Wv_scales, 
         bias = const.tile([P, DV], BF16)
 
         def spread_bias():
-            for h in range(HALVES):
-                half = slice(BANK * h, BANK * (h + 1))
+            for first in range(0, DV, BANK):
                 spread = psum.tile([P, BANK], F32, tag="bank")
-                nc.tensor.matmul(out=spread[:], lhsT=ones[:], rhs=bias_row[:, half], start=True, stop=True)
-                nc.scalar.copy(out=bias[:, half], in_=spread[:])
+                nc.tensor.matmul(
+                    out=spread[:], lhsT=ones[:], rhs=bias_row[:, first : first + BANK], start=True, stop=True
+                )
+                nc.scalar.copy(out=bias[:, first : first + BANK], in_=spread[:])
 
         def load_rows(rows, row_tiles, name):
             tile = rows_pool.tile([P, row_tiles, D], BF16, name=name)
@@ -215,8 +217,8 @@ def tile_bottleneck_attention_pa_kernel(tc, qp_top, kp, v, Wv_words, Wv_scales, 
                 quantise_pair(grouped[pair], v_mx[0][:, pair], v_mx[1][:, pair])
             return v_mx
 
-        def project_chunk(h, c, v_mx, vp_grouped):
-            features = slice(BANK * h + P * c, BANK * h + P * (c + 1))
+        def project_chunk(u, c, v_mx, vp_grouped):
+            features = slice(UNIT * u + P * c, UNIT * u + P * (c + 1))
             quad = multiply_quad(v_mx, lambda g: (w_words[:, g, features], w_scales[:, g, features]))
             nc.vector.tensor_tensor(
                 out=vp_grouped[:, P * c : P * (c + 1), :],
@@ -225,30 +227,30 @@ def tile_bottleneck_attention_pa_kernel(tc, qp_top, kp, v, Wv_words, Wv_scales, 
                 op=ALU.add,
             )
 
-        def quantise_projection(b, h, vp_grouped):
-            half = slice(BANK * h, BANK * (h + 1))
+        def quantise_projection(b, u, vp_grouped):
+            features = slice(UNIT * u, UNIT * (u + 1))
             nc.vector.quantize_mx(
-                out=vp_codes[b][:, half].bitcast(FP8X4),
-                scales=vp_scales[b][:, half],
+                out=vp_codes[b][:, features].bitcast(FP8X4),
+                scales=vp_scales[b][:, features],
                 in_=vp_grouped[:].rearrange("p n t -> p (n t)"),
             )
 
-        def attend(b, h, copies):
-            half = slice(BANK * h, BANK * (h + 1))
-            result = store_pool.tile([P, Q_TILES, BANK], F32)
+        def attend(b, u):
+            features = slice(UNIT * u, UNIT * (u + 1))
+            acc = psum.tile([P, Q_TILES, UNIT], F32, tag="bank")
             for s in both:
-                acc = psum.tile([P, BANK], F32, tag="bank")
                 nc.tensor.matmul_mx(
-                    out=acc[:],
+                    out=acc[:, s, :],
                     lhsT=attn_codes[s][:, b, :].bitcast(FP8X4),
                     lhsT_scale=attn_scales[s][:, b, :],
-                    rhs=vp_codes[b][:, half].bitcast(FP8X4),
-                    rhs_scale=vp_scales[b][:, half],
+                    rhs=vp_codes[b][:, features].bitcast(FP8X4),
+                    rhs_scale=vp_scales[b][:, features],
                     start=True,
                     stop=True,
                 )
-                copies[s](out=result[:, s, :], in_=acc[:])
-            nc.sync.dma_start(out=out[b].rearrange("(p s) n -> p s n", s=Q_TILES)[:, :, half], in_=result[:])
+            result = store_pool.tile([P, Q_TILES, UNIT], F32)
+            nc.scalar.copy(out=result[:], in_=acc[:])
+            nc.sync.dma_start(out=out[b].rearrange("(p s) n -> p s n", s=Q_TILES)[:, :, features], in_=result[:])
 
         grouped = turn_queries_and_keys(0)
         for b in range(B):
@@ -268,25 +270,23 @@ def tile_bottleneck_attention_pa_kernel(tc, qp_top, kp, v, Wv_words, Wv_scales, 
         v_mx[1] = quantise_values(v_grouped[1])
         v_grouped[2] = turn_values(2)
 
-        both_scalar = (nc.scalar.copy, nc.scalar.copy)
-        scalar_and_vector = (nc.scalar.copy, nc.vector.tensor_copy)
-        halves = [(b, h) for b in range(B) for h in range(HALVES)]
+        units = [(b, u) for b in range(B) for u in range(UNITS)]
         vp_grouped = {}
-        for n, (b, h) in enumerate(halves):
-            vp_grouped[n] = group_pool.tile([P, BANK, PACK], BF16, name="vp_grouped%d" % n, tag="vp_grouped", align_bytes=64)
+        for n, (b, u) in enumerate(units):
+            vp_grouped[n] = group_pool.tile([P, UNIT, PACK], BF16, name="vp_grouped%d" % n, tag="vp_grouped", bufs=4, align_bytes=64)
             for c in range(CHUNKS):
-                project_chunk(h, c, v_mx[b], vp_grouped[n])
+                project_chunk(u, c, v_mx[b], vp_grouped[n])
                 if c == 0 and n > 0:
-                    quantise_projection(halves[n - 1][0], halves[n - 1][1], vp_grouped[n - 1])
-            if h == HALVES - 1 and b + 2 < B:
+                    quantise_projection(units[n - 1][0], units[n - 1][1], vp_grouped[n - 1])
+            if u == UNITS - 1 and b + 2 < B:
                 if b == 0:
                     weights(inverse)
                 v_mx[b + 2] = quantise_values(v_grouped[b + 2])
                 if b + 3 < B:
                     v_grouped[b + 3] = turn_values(b + 3)
             if b >= 2:
-                for i in range(2 * (n - 2 * HALVES), 2 * (n - 2 * HALVES) + 2):
+                for i in range(2 * (n - 2 * UNITS), 2 * (n - 2 * UNITS) + 2):
                     if i < n:
-                        attend(halves[i][0], halves[i][1], both_scalar)
-        quantise_projection(B - 1, HALVES - 1, vp_grouped[len(halves) - 1])
-        attend(B - 1, HALVES - 1, scalar_and_vector)
+                        attend(units[i][0], units[i][1])
+        quantise_projection(B - 1, UNITS - 1, vp_grouped[len(units) - 1])
+        attend(B - 1, UNITS - 1)

@@ -24,7 +24,8 @@ BANK = 512
 UNIT = BANK // Q_TILES
 UNITS = DV // UNIT
 CHUNKS = UNIT // P
-PSUM_BANKS = 8
+PASSING_BANKS = 6
+HELD_BANKS = 2
 GROUPED_BUFS = 6
 
 FLOPS = 2 * B * (L * D * DV + BN * L * D + BN * L * DV)
@@ -40,7 +41,8 @@ def tile_bottleneck_attention_pa_kernel(tc, qp_top, kp, v, Wv_words, Wv_scales, 
         keep = ctx.enter_context(tc.tile_pool(name="keep", bufs=1))
         soft = ctx.enter_context(tc.tile_pool(name="soft", bufs=2))
         store_pool = ctx.enter_context(tc.tile_pool(name="store", bufs=6))
-        psum = ctx.enter_context(tc.psum_pool(name="psum", bufs=PSUM_BANKS))
+        psum = ctx.enter_context(tc.psum_pool(name="psum", bufs=1))
+        ctx.enter_context(tc.manual_schedule())
 
         ident = const.tile([P, P], F32)
         make_identity(nc, ident[:])
@@ -53,10 +55,18 @@ def tile_bottleneck_attention_pa_kernel(tc, qp_top, kp, v, Wv_words, Wv_scales, 
         ones = const.tile([P, P], BF16)
         nc.vector.memset(ones[:], 1.0)
         bias = const.tile([P, DV], BF16)
+        w_scales = const.tile([P, PASSES, DV], U8, align_bytes=64)
+        nc.vector.memset(w_scales[:].bitcast(I32), 0)
+
+        def passing_bank(shape):
+            return psum.tile(shape, F32, name="passing", tag="passing", bufs=PASSING_BANKS)
+
+        def held_bank(shape):
+            return psum.tile(shape, F32, name="held", tag="held", bufs=HELD_BANKS)
 
         def spread_bias():
             for first in range(0, DV, BANK):
-                spread = psum.tile([P, BANK], F32, tag="bank")
+                spread = passing_bank([P, BANK])
                 nc.tensor.matmul(
                     out=spread[:], lhsT=ones[:], rhs=bias_row[:, first : first + BANK], start=True, stop=True
                 )
@@ -74,10 +84,8 @@ def tile_bottleneck_attention_pa_kernel(tc, qp_top, kp, v, Wv_words, Wv_scales, 
         for b in range(B):
             query_rows.append(load_rows(qp_top[b], Q_TILES, "q_rows%d" % b))
             key_rows.append(load_rows(kp[b], PACK, "k_rows%d" % b))
-
+        value_rows = [load_rows(v[0], PACK, "v_rows0")]
         nc.sync.dma_start(out=bias_row[0:1, :], in_=bv.unsqueeze(0))
-        w_scales = const.tile([P, PASSES, DV], U8, align_bytes=64)
-        nc.vector.memset(w_scales[:].bitcast(I32), 0)
         for quadrant in range(4):
             nc.sync.dma_start(
                 out=w_scales[32 * quadrant : 32 * quadrant + 4, :, :].bitcast(I32),
@@ -88,14 +96,15 @@ def tile_bottleneck_attention_pa_kernel(tc, qp_top, kp, v, Wv_words, Wv_scales, 
             out=w_words[:].bitcast(I32),
             in_=Wv_words.rearrange("g p n t -> p g (n t)").bitcast(I32),
         )
-        value_rows = [load_rows(v[b], PACK, "v_rows%d" % b) for b in range(B)]
+        for b in range(1, B):
+            value_rows.append(load_rows(v[b], PACK, "v_rows%d" % b))
 
         def turn_pair(rows, first, as_weight, copy):
             words = rows[:].bitcast(F32)
             grouped = group_pool.tile([P, PASSES, PAIR * P, PACK], BF16, tag="grouped", bufs=GROUPED_BUFS, align_bytes=64)
             step = 2 if as_weight else 1
             for t in range(PAIR):
-                turned = psum.tile([P, PASSES, 2, P], F32, tag="bank")
+                turned = passing_bank([P, PASSES, 2, P])
                 for g in range(PASSES):
                     for u in range(2):
                         start = WORDS * g + (u if as_weight else P * u)
@@ -122,8 +131,8 @@ def tile_bottleneck_attention_pa_kernel(tc, qp_top, kp, v, Wv_words, Wv_scales, 
             scales = code_pool.tile([P, pairs, PASSES, PAIR * P], U8, tag=tag + "_scales", align_bytes=64)
             return codes, scales
 
-        def multiply_quad(keys_mx, moving_of_pass):
-            acc = psum.tile([P, PACK, P], F32, tag="bank")
+        def multiply_quad(keys_mx, moving_of_pass, new_bank):
+            acc = new_bank([P, PACK, P])
             for t in range(PACK):
                 rows = slice(P * (t % PAIR), P * (t % PAIR + 1))
                 for g in range(PASSES):
@@ -140,7 +149,9 @@ def tile_bottleneck_attention_pa_kernel(tc, qp_top, kp, v, Wv_words, Wv_scales, 
             return acc[:].rearrange("p t c -> p c t")
 
         width = P * PACK
-        score = [keep.tile([P, B, width], F32, name="score%d" % s) for s in range(Q_TILES)]
+        both = range(Q_TILES)
+        score = [keep.tile([P, B, width], F32, name="score%d" % s) for s in both]
+        last_scores = []
 
         def turn_queries_and_keys(b):
             return [turn_pair(query_rows[b], 0, False, nc.vector.tensor_copy)] + [
@@ -156,54 +167,62 @@ def tile_bottleneck_attention_pa_kernel(tc, qp_top, kp, v, Wv_words, Wv_scales, 
             return q_mx, k_mx
 
         def scores(b, q_mx, k_mx):
-            for s in range(Q_TILES):
+            for s in both:
                 queries = slice(P * s, P * (s + 1))
-                quad = multiply_quad(k_mx, lambda g: (q_mx[0][:, 0, g, queries], q_mx[1][:, 0, g, queries]))
-                nc.scalar.copy(out=score[s][:, b, :].rearrange("p (i t) -> p i t", t=PACK), in_=quad)
+                quad = multiply_quad(
+                    k_mx, lambda g: (q_mx[0][:, 0, g, queries], q_mx[1][:, 0, g, queries]), held_bank
+                )
+                if b == B - 1:
+                    last_scores.append(quad)
+                else:
+                    nc.scalar.copy(out=score[s][:, b, :].rearrange("p (i t) -> p i t", t=PACK), in_=quad)
 
-        over_b = [P, B, width]
-        both = range(Q_TILES)
+        top = [soft.tile([P, width], F32, name="top%d" % s, tag="single", bufs=4) for s in both]
+        total = [soft.tile([P, width], F32, name="total%d" % s, tag="single", bufs=4) for s in both]
         attn_codes = [keep.tile([P, B, P], U32, name="attn_codes%d" % s, align_bytes=64) for s in both]
         attn_scales = [keep.tile([P, B, P], U8, name="attn_scales%d" % s, align_bytes=64) for s in both]
 
-        def over_batch(op, name):
-            folded = [soft.tile([P, width], F32, name="%s%d" % (name, s), tag="single", bufs=4) for s in both]
-            for b in range(1, B):
-                for s in both:
-                    so_far = score[s][:, 0, :] if b == 1 else folded[s][:]
-                    nc.vector.tensor_tensor(out=folded[s][:], in0=so_far, in1=score[s][:, b, :], op=op)
-            return folded
+        def as_quad(flat):
+            return flat.rearrange("p (i t) -> p i t", t=PACK)
 
-        def exp_of_shifted():
-            top = over_batch(ALU.max, "top")
+        def fold(folded, b, op):
             for s in both:
-                x = score[s]
-                nc.vector.tensor_tensor(
-                    out=x[:], in0=x[:], in1=top[s][:].unsqueeze(1).to_broadcast(over_b), op=ALU.subtract
-                )
-                nc.scalar.activation(out=x[:], in_=x[:], func=ACT.Exp, scale=1.0 / 32.0)
+                so_far = score[s][:, 0, :] if b == 1 else folded[s][:]
+                nc.vector.tensor_tensor(out=folded[s][:], in0=so_far, in1=score[s][:, b, :], op=op)
 
-        def inverse_of(total):
-            logs = [soft.tile([P, width], F32, name="log%d" % s, tag="single", bufs=4) for s in both]
+        def fold_top_of_last():
+            for s in both:
+                nc.vector.tensor_tensor(out=as_quad(top[s][:]), in0=last_scores[s], in1=as_quad(top[s][:]), op=ALU.max)
+
+        def shift_and_exp(b):
+            for s in both:
+                x = score[s][:, b, :]
+                if b == B - 1:
+                    nc.vector.tensor_tensor(
+                        out=as_quad(x), in0=last_scores[s], in1=as_quad(top[s][:]), op=ALU.subtract
+                    )
+                else:
+                    nc.vector.tensor_tensor(out=x, in0=x, in1=top[s][:], op=ALU.subtract)
+                nc.scalar.activation(out=x, in_=x, func=ACT.Exp, scale=1.0 / 32.0)
+
+        def inverse_of_total():
+            logs = [soft.tile([P, width], F32, name="log%d" % s, tag="log", bufs=2) for s in both]
             for s in both:
                 nc.scalar.activation(out=logs[s][:], in_=total[s][:], func=ACT.Ln)
-            inverse = [soft.tile([P, width], F32, name="inverse%d" % s, tag="single", bufs=4) for s in both]
+            inverse = [soft.tile([P, width], F32, name="inverse%d" % s, tag="inverse", bufs=2) for s in both]
             for s in both:
                 nc.scalar.activation(out=inverse[s][:], in_=logs[s][:], func=ACT.Exp, scale=-1.0)
             return inverse
 
-        def weights(inverse):
-            attn = [soft.tile([P, B, width], BF16, name="attn%d" % s, tag="attn", align_bytes=64) for s in both]
-            for s in both:
-                nc.vector.tensor_tensor(
-                    out=attn[s][:], in0=score[s][:], in1=inverse[s][:].unsqueeze(1).to_broadcast(over_b), op=ALU.mult
-                )
-            for s in both:
-                nc.vector.quantize_mx(
-                    out=attn_codes[s][:].rearrange("p b i -> p (b i)").bitcast(FP8X4),
-                    scales=attn_scales[s][:].rearrange("p b i -> p (b i)"),
-                    in_=attn[s][:].rearrange("p b c -> p (b c)"),
-                )
+        def weights(b, s, inverse):
+            attn = soft.tile([P, width], BF16, name="attn", tag="attn", bufs=1, align_bytes=64)
+            nc.gpsimd.tensor_tensor(out=attn[:], in0=score[s][:, b, :], in1=inverse[s][:], op=ALU.mult)
+            return attn
+
+        def quantise_weights(b, s, attn):
+            nc.vector.quantize_mx(
+                out=attn_codes[s][:, b, :].bitcast(FP8X4), scales=attn_scales[s][:, b, :], in_=attn[:]
+            )
 
         vp_codes = [keep.tile([P, DV], U32, name="vp_codes%d" % b, align_bytes=64) for b in range(B)]
         vp_scales = [keep.tile([P, DV], U8, name="vp_scales%d" % b, align_bytes=64) for b in range(B)]
@@ -219,7 +238,7 @@ def tile_bottleneck_attention_pa_kernel(tc, qp_top, kp, v, Wv_words, Wv_scales, 
 
         def project_chunk(u, c, v_mx, vp_grouped):
             features = slice(UNIT * u + P * c, UNIT * u + P * (c + 1))
-            quad = multiply_quad(v_mx, lambda g: (w_words[:, g, features], w_scales[:, g, features]))
+            quad = multiply_quad(v_mx, lambda g: (w_words[:, g, features], w_scales[:, g, features]), passing_bank)
             nc.vector.tensor_tensor(
                 out=vp_grouped[:, P * c : P * (c + 1), :],
                 in0=quad,
@@ -227,17 +246,19 @@ def tile_bottleneck_attention_pa_kernel(tc, qp_top, kp, v, Wv_words, Wv_scales, 
                 op=ALU.add,
             )
 
-        def quantise_projection(b, u, vp_grouped):
+        def quantise_projection(n):
+            b, u = units[n]
             features = slice(UNIT * u, UNIT * (u + 1))
             nc.vector.quantize_mx(
                 out=vp_codes[b][:, features].bitcast(FP8X4),
                 scales=vp_scales[b][:, features],
-                in_=vp_grouped[:].rearrange("p n t -> p (n t)"),
+                in_=vp_grouped[n][:].rearrange("p n t -> p (n t)"),
             )
 
-        def attend(b, u):
+        def attend(n):
+            b, u = units[n]
             features = slice(UNIT * u, UNIT * (u + 1))
-            acc = psum.tile([P, Q_TILES, UNIT], F32, tag="bank")
+            acc = held_bank([P, Q_TILES, UNIT])
             for s in both:
                 nc.tensor.matmul_mx(
                     out=acc[:, s, :],
@@ -252,41 +273,63 @@ def tile_bottleneck_attention_pa_kernel(tc, qp_top, kp, v, Wv_words, Wv_scales, 
             nc.scalar.copy(out=result[:], in_=acc[:])
             nc.sync.dma_start(out=out[b].rearrange("(p s) n -> p s n", s=Q_TILES)[:, :, features], in_=result[:])
 
+        units = [(b, u) for b in range(B) for u in range(UNITS)]
+        vp_grouped = {}
+
+        def project_unit(n, between=None):
+            b, u = units[n]
+            vp_grouped[n] = group_pool.tile([P, UNIT, PACK], BF16, name="vp_grouped%d" % n, tag="vp_grouped", bufs=4, align_bytes=64)
+            for c in range(CHUNKS):
+                project_chunk(u, c, v_mx[b], vp_grouped[n])
+                if c == 0 and n > 0:
+                    quantise_projection(n - 1)
+                if c == 0 and between is not None:
+                    between()
+
+        v_mx = {}
+        v_grouped = {}
         grouped = turn_queries_and_keys(0)
         for b in range(B):
             q_mx, k_mx = quantise_queries_and_keys(grouped)
             if b + 1 < B:
                 grouped = turn_queries_and_keys(b + 1)
             scores(b, q_mx, k_mx)
-
+            if b >= 2:
+                fold(top, b - 1, ALU.max)
+        v_grouped[0] = turn_values(0)
+        fold_top_of_last()
+        shift_and_exp(3)
+        v_mx[0] = quantise_values(v_grouped[0])
         spread_bias()
-        v_grouped = {}
-        for b in range(2):
-            v_grouped[b] = turn_values(b)
-        exp_of_shifted()
-        v_mx = {0: quantise_values(v_grouped[0])}
-        total = over_batch(ALU.add, "total")
-        inverse = inverse_of(total)
+        for b in (0, 1, 2):
+            shift_and_exp(b)
+        project_unit(0)
+        v_grouped[1] = turn_values(1)
+        for b in range(1, B):
+            fold(total, b, ALU.add)
+        project_unit(1)
+        project_unit(2)
         v_mx[1] = quantise_values(v_grouped[1])
         v_grouped[2] = turn_values(2)
-
-        units = [(b, u) for b in range(B) for u in range(UNITS)]
-        vp_grouped = {}
-        for n, (b, u) in enumerate(units):
-            vp_grouped[n] = group_pool.tile([P, UNIT, PACK], BF16, name="vp_grouped%d" % n, tag="vp_grouped", bufs=4, align_bytes=64)
-            for c in range(CHUNKS):
-                project_chunk(u, c, v_mx[b], vp_grouped[n])
-                if c == 0 and n > 0:
-                    quantise_projection(units[n - 1][0], units[n - 1][1], vp_grouped[n - 1])
-            if u == UNITS - 1 and b + 2 < B:
-                if b == 0:
-                    weights(inverse)
-                v_mx[b + 2] = quantise_values(v_grouped[b + 2])
-                if b + 3 < B:
-                    v_grouped[b + 3] = turn_values(b + 3)
-            if b >= 2:
-                for i in range(2 * (n - 2 * UNITS), 2 * (n - 2 * UNITS) + 2):
-                    if i < n:
-                        attend(units[i][0], units[i][1])
-        quantise_projection(B - 1, UNITS - 1, vp_grouped[len(units) - 1])
-        attend(B - 1, UNITS - 1)
+        inverse = inverse_of_total()
+        project_unit(3)
+        project_unit(4)
+        v_mx[2] = quantise_values(v_grouped[2])
+        v_grouped[3] = turn_values(3)
+        done = 0
+        for i in range(11):
+            if i < 2 * B:
+                b, s = divmod(i, 2)
+                attn = weights(b, s, inverse)
+                project_unit(5 + i, lambda: quantise_weights(b, s, attn))
+            else:
+                project_unit(5 + i)
+            if i == 3:
+                v_mx[3] = quantise_values(v_grouped[3])
+            ready = min(4 * ((i - 1) // 2), i + 4)
+            for n in range(done, min(done + 2, ready)):
+                attend(n)
+                done = n + 1
+        quantise_projection(15)
+        for n in range(done, 16):
+            attend(n)

@@ -215,8 +215,8 @@ def tile_bottleneck_attention_pa_kernel(tc, qp_top, kp, v, Wv_words, Wv_scales, 
             return inverse
 
         def weights(b, s, inverse):
-            attn = soft.tile([P, width], BF16, name="attn", tag="attn", bufs=1, align_bytes=64)
-            nc.gpsimd.tensor_tensor(out=attn[:], in0=score[s][:, b, :], in1=inverse[s][:], op=ALU.mult)
+            attn = soft.tile([P, width], BF16, name="attn", tag="attn", bufs=2, align_bytes=64)
+            nc.vector.tensor_tensor(out=attn[:], in0=score[s][:, b, :], in1=inverse[s][:], op=ALU.mult)
             return attn
 
         def quantise_weights(b, s, attn):

@@ -28,6 +28,16 @@ PASSING_BANKS = 6
 HELD_BANKS = 2
 GROUPED_BUFS = 6
 
+ROW_BUFS = (0, 4, 6)
+FEATURE_TILES = DV // P
+STATIONARY = (0, 1, 3)
+SEQUENCE = (0, 1, 2, 3)
+UNIT_ORDER = [(0, 0), (0, 1), (0, 2), (0, 3), (1, 0), (1, 1), (1, 2), (1, 3), (2, 0), (2, 1), (2, 2), (2, 3), (3, 0), (3, 1), (3, 2), (3, 3)]
+TURN_LAST = 0
+QUANT_LAST = 3
+BIAS_ON_VECTOR = ()
+WORDS_ON_VECTOR = ()
+
 FLOPS = 2 * B * (L * D * DV + BN * L * D + BN * L * DV)
 
 
@@ -42,7 +52,6 @@ def tile_bottleneck_attention_pa_kernel(tc, qp_top, kp, v, Wv_words, Wv_scales, 
         soft = ctx.enter_context(tc.tile_pool(name="soft", bufs=2))
         store_pool = ctx.enter_context(tc.tile_pool(name="store", bufs=6))
         psum = ctx.enter_context(tc.psum_pool(name="psum", bufs=1))
-        ctx.enter_context(tc.manual_schedule())
 
         ident = const.tile([P, P], F32)
         make_identity(nc, ident[:])
@@ -52,6 +61,11 @@ def tile_bottleneck_attention_pa_kernel(tc, qp_top, kp, v, Wv_words, Wv_scales, 
 
         bias_row = const.tile([P, DV], BF16)
         nc.vector.memset(bias_row[:].bitcast(I32), 0)
+        bias_rows = const.tile([P, P], BF16)
+        nc.vector.memset(bias_rows[:].bitcast(I32), 0)
+        ident_rows = const.tile([P, P], BF16)
+        nc.vector.tensor_copy(out=ident_rows[:], in_=ident[:])
+        bias_column = const.tile([P, FEATURE_TILES], F32)
         ones = const.tile([P, P], BF16)
         nc.vector.memset(ones[:], 1.0)
         bias = const.tile([P, DV], BF16)
@@ -72,20 +86,43 @@ def tile_bottleneck_attention_pa_kernel(tc, qp_top, kp, v, Wv_words, Wv_scales, 
                 )
                 nc.scalar.copy(out=bias[:, first : first + BANK], in_=spread[:])
 
-        def load_rows(rows, row_tiles, name):
-            tile = rows_pool.tile([P, row_tiles, D], BF16, name=name)
-            by_partition = rows.rearrange("(p t) d -> p t d", t=row_tiles)
-            for first in range(0, row_tiles, PAIR):
-                nc.sync.dma_start(out=tile[:, first : first + PAIR, :], in_=by_partition[:, first : first + PAIR, :])
+            column = passing_bank([P, FEATURE_TILES])
+            nc.tensor.matmul(
+                out=column[:], lhsT=bias_rows[:], rhs=ident_rows[:, 0:FEATURE_TILES], start=True, stop=True
+            )
+            nc.scalar.copy(out=bias_column[:], in_=column[:])
+
+        def load_rows(rows, pair_of, name):
+            pairs = rows.shape[0] // P // PAIR
+            tile = rows_pool.tile([P, pairs * PAIR, D], BF16, name=name, tag="rows%d" % pairs, bufs=ROW_BUFS[pairs])
+            for i in range(pairs):
+                nc.sync.dma_start(out=tile[:, PAIR * i : PAIR * (i + 1), :], in_=pair_of(rows, i))
             return tile
+
+        def query_pair(rows, i):
+            return rows.rearrange("(p s) d -> p s d", s=Q_TILES)
+
+        def key_pair(rows, i):
+            return rows.rearrange("(u p e) d -> u p e d", p=P, e=PAIR)[i]
+
+        def plain_pair(rows, i):
+            return rows.rearrange("(t p) d -> p t d", p=P)[:, PAIR * i : PAIR * (i + 1), :]
+
+        def is_stationary(b):
+            return b in STATIONARY
+
+        def load_values(b):
+            value_rows[b] = load_rows(v[b], key_pair if is_stationary(b) else plain_pair, "v_rows%d" % b)
 
         query_rows = []
         key_rows = []
         for b in range(B):
-            query_rows.append(load_rows(qp_top[b], Q_TILES, "q_rows%d" % b))
-            key_rows.append(load_rows(kp[b], PACK, "k_rows%d" % b))
-        value_rows = [load_rows(v[0], PACK, "v_rows0")]
+            query_rows.append(load_rows(qp_top[b], query_pair, "q_rows%d" % b))
+            key_rows.append(load_rows(kp[b], key_pair, "k_rows%d" % b))
+        value_rows = {}
+        load_values(SEQUENCE[0])
         nc.sync.dma_start(out=bias_row[0:1, :], in_=bv.unsqueeze(0))
+        nc.sync.dma_start(out=bias_rows[0:FEATURE_TILES, :], in_=bv.rearrange("(f p) -> f p", p=P))
         for quadrant in range(4):
             nc.sync.dma_start(
                 out=w_scales[32 * quadrant : 32 * quadrant + 4, :, :].bitcast(I32),
@@ -96,8 +133,8 @@ def tile_bottleneck_attention_pa_kernel(tc, qp_top, kp, v, Wv_words, Wv_scales, 
             out=w_words[:].bitcast(I32),
             in_=Wv_words.rearrange("g p n t -> p g (n t)").bitcast(I32),
         )
-        for b in range(1, B):
-            value_rows.append(load_rows(v[b], PACK, "v_rows%d" % b))
+        for b in SEQUENCE[1:]:
+            load_values(b)
 
         def turn_pair(rows, first, as_weight, copy):
             words = rows[:].bitcast(F32)
@@ -228,13 +265,68 @@ def tile_bottleneck_attention_pa_kernel(tc, qp_top, kp, v, Wv_words, Wv_scales, 
         vp_scales = [keep.tile([P, DV], U8, name="vp_scales%d" % b, align_bytes=64) for b in range(B)]
 
         def turn_values(b):
-            return [turn_pair(value_rows[b], first, True, nc.scalar.copy) for first in range(0, PACK, PAIR)]
+            if is_stationary(b):
+                return [turn_pair(value_rows[b], first, True, nc.scalar.copy) for first in range(0, PACK, PAIR)]
+            words = value_rows[b][:].bitcast(F32)
+            grouped = group_pool.tile([P, PASSES, L, PACK], BF16, tag="grouped_moving", bufs=1, align_bytes=64)
+            for t in range(PACK):
+                turned = passing_bank([P, PASSES, 2, P])
+                for g in range(PASSES):
+                    for u in range(2):
+                        start = WORDS * g + u
+                        nc.tensor.transpose(
+                            turned[:, g, u, :], words[:, t, start : start + 2 * (P - 1) + 1 : 2], ident[:]
+                        )
+                nc.scalar.copy(
+                    out=grouped[:].bitcast(F32)[:, :, P * t : P * (t + 1), :],
+                    in_=turned[:].rearrange("p g u r -> p g r u"),
+                )
+            return grouped
 
-        def quantise_values(grouped):
+        def quantise_values(b, grouped):
             v_mx = new_codes(PACK // PAIR, "v")
-            for pair in range(PACK // PAIR):
-                quantise_pair(grouped[pair], v_mx[0][:, pair], v_mx[1][:, pair])
-            return v_mx
+            if is_stationary(b):
+                for pair in range(PACK // PAIR):
+                    quantise_pair(grouped[pair], v_mx[0][:, pair], v_mx[1][:, pair])
+                return v_mx
+            codes = v_mx[0][:].rearrange("p a g c -> p (a g c)").rearrange("p (g c) -> p g c", g=PASSES)
+            scales = v_mx[1][:].rearrange("p a g c -> p (a g c)").rearrange("p (g c) -> p g c", g=PASSES)
+            for g in range(PASSES):
+                nc.vector.quantize_mx(
+                    out=codes[:, g].bitcast(FP8X4),
+                    scales=scales[:, g],
+                    in_=grouped[:, g].rearrange("p c f -> p (c f)"),
+                )
+            return codes, scales
+
+        def project_tile(b, f, codes, scales, turned_vp, half):
+            features = slice(P * f, P * (f + 1))
+            acc = passing_bank([P, L])
+            for g in range(PASSES):
+                nc.tensor.matmul_mx(
+                    out=acc[:],
+                    lhsT=w_words[:, g, features].bitcast(FP8X4),
+                    lhsT_scale=w_scales[:, g, features],
+                    rhs=codes[:, g].bitcast(FP8X4),
+                    rhs_scale=scales[:, g],
+                    start=(g == 0),
+                    stop=(g == PASSES - 1),
+                )
+            if (b, f) in BIAS_ON_VECTOR:
+                nc.vector.tensor_scalar(out=turned_vp[:, half, :], in0=acc[:], scalar1=bias_column[:, f : f + 1], scalar2=None, op0=ALU.add)
+            else:
+                nc.scalar.activation(out=turned_vp[:, half, :], in_=acc[:], func=ACT.Identity, bias=bias_column[:, f : f + 1])
+
+        def turn_projection(b, u):
+            words = turned_vp[b, u][:].bitcast(F32)
+            bank = passing_bank([P, CHUNKS, 2, P])
+            for c in range(CHUNKS):
+                for h in range(2):
+                    nc.tensor.transpose(bank[:, c, h, :], words[:, c, P * h : P * (h + 1)], ident[:])
+            (nc.vector.tensor_copy if (b, u) in WORDS_ON_VECTOR else nc.scalar.copy)(
+                out=vp_grouped[b, u][:].bitcast(F32).rearrange("p (c n) h -> p c n h", c=CHUNKS),
+                in_=bank[:].rearrange("p c h n -> p c n h"),
+            )
 
         def project_chunk(u, c, v_mx, vp_grouped):
             features = slice(UNIT * u + P * c, UNIT * u + P * (c + 1))
@@ -246,17 +338,15 @@ def tile_bottleneck_attention_pa_kernel(tc, qp_top, kp, v, Wv_words, Wv_scales, 
                 op=ALU.add,
             )
 
-        def quantise_projection(n):
-            b, u = units[n]
+        def quantise_projection(b, u):
             features = slice(UNIT * u, UNIT * (u + 1))
             nc.vector.quantize_mx(
                 out=vp_codes[b][:, features].bitcast(FP8X4),
                 scales=vp_scales[b][:, features],
-                in_=vp_grouped[n][:].rearrange("p n t -> p (n t)"),
+                in_=vp_grouped[b, u][:].rearrange("p n t -> p (n t)"),
             )
 
-        def attend(n):
-            b, u = units[n]
+        def attend(b, u):
             features = slice(UNIT * u, UNIT * (u + 1))
             acc = held_bank([P, Q_TILES, UNIT])
             for s in both:
@@ -273,21 +363,32 @@ def tile_bottleneck_attention_pa_kernel(tc, qp_top, kp, v, Wv_words, Wv_scales, 
             nc.scalar.copy(out=result[:], in_=acc[:])
             nc.sync.dma_start(out=out[b].rearrange("(p s) n -> p s n", s=Q_TILES)[:, :, features], in_=result[:])
 
-        units = [(b, u) for b in range(B) for u in range(UNITS)]
         vp_grouped = {}
+        turned_vp = {}
 
-        def project_unit(n, between=None):
-            b, u = units[n]
-            vp_grouped[n] = group_pool.tile([P, UNIT, PACK], BF16, name="vp_grouped%d" % n, tag="vp_grouped", bufs=4, align_bytes=64)
+        def project_unit(b, u, between):
+            vp_grouped[b, u] = group_pool.tile([P, UNIT, PACK], BF16, name="vp_grouped%d_%d" % (b, u), tag="vp_grouped", bufs=4, align_bytes=64)
+            if not is_stationary(b):
+                turned_vp[b, u] = group_pool.tile([P, CHUNKS, L], BF16, name="turned_vp%d_%d" % (b, u), tag="turned_vp", bufs=3, align_bytes=64)
             for c in range(CHUNKS):
-                project_chunk(u, c, v_mx[b], vp_grouped[n])
-                if c == 0 and n > 0:
-                    quantise_projection(n - 1)
-                if c == 0 and between is not None:
-                    between()
+                if is_stationary(b):
+                    project_chunk(u, c, v_mx[b], vp_grouped[b, u])
+                else:
+                    project_tile(b, CHUNKS * u + c, v_mx[b][0], v_mx[b][1], turned_vp[b, u], c)
+                if c == 0:
+                    for work in between:
+                        work()
 
         v_mx = {}
         v_grouped = {}
+
+        def turn_next(i):
+            v_grouped[SEQUENCE[i]] = turn_values(SEQUENCE[i])
+
+        def quantise_next(i):
+            b = SEQUENCE[i]
+            v_mx[b] = quantise_values(b, v_grouped[b])
+
         grouped = turn_queries_and_keys(0)
         for b in range(B):
             q_mx, k_mx = quantise_queries_and_keys(grouped)
@@ -296,40 +397,60 @@ def tile_bottleneck_attention_pa_kernel(tc, qp_top, kp, v, Wv_words, Wv_scales, 
             scores(b, q_mx, k_mx)
             if b >= 2:
                 fold(top, b - 1, ALU.max)
-        v_grouped[0] = turn_values(0)
+        turn_next(0)
         fold_top_of_last()
         shift_and_exp(3)
-        v_mx[0] = quantise_values(v_grouped[0])
+        quantise_next(0)
         spread_bias()
         for b in (0, 1, 2):
             shift_and_exp(b)
-        project_unit(0)
-        v_grouped[1] = turn_values(1)
+
+        later = {}
+        ready = []
+
+        def after(step, work):
+            later.setdefault(step, []).append(work)
+
+        def run(step, extra=None):
+            b, u = UNIT_ORDER[step]
+            project_unit(b, u, later.get(step, []) + ([extra] if extra else []))
+            if is_stationary(b):
+                after(step + 1, lambda: quantise_projection(b, u))
+                ready.append((max(step + 3, 8 + 2 * b), b, u))
+            else:
+                after(step + 1, lambda: turn_projection(b, u))
+                after(step + 2, lambda: quantise_projection(b, u))
+                ready.append((max(step + 4, 8 + 2 * b), b, u))
+
+        def attend_ready(step, most):
+            for entry in [e for e in ready if e[0] <= step][:most]:
+                attend(entry[1], entry[2])
+                ready.remove(entry)
+
+        run(0)
+        turn_next(1)
         for b in range(1, B):
             fold(total, b, ALU.add)
-        project_unit(1)
-        project_unit(2)
-        v_mx[1] = quantise_values(v_grouped[1])
-        v_grouped[2] = turn_values(2)
+        run(1)
+        run(2)
+        quantise_next(1)
+        turn_next(2)
         inverse = inverse_of_total()
-        project_unit(3)
-        project_unit(4)
-        v_mx[2] = quantise_values(v_grouped[2])
-        v_grouped[3] = turn_values(3)
-        done = 0
+        run(3)
+        run(4)
+        quantise_next(2)
+        turn_next(3)
         for i in range(11):
             if i < 2 * B:
                 b, s = divmod(i, 2)
                 attn = weights(b, s, inverse)
-                project_unit(5 + i, lambda: quantise_weights(b, s, attn))
+                run(5 + i, lambda: quantise_weights(b, s, attn))
             else:
-                project_unit(5 + i)
-            if i == 3:
-                v_mx[3] = quantise_values(v_grouped[3])
-            ready = min(4 * ((i - 1) // 2), i + 4)
-            for n in range(done, min(done + 2, ready)):
-                attend(n)
-                done = n + 1
-        quantise_projection(15)
-        for n in range(done, 16):
-            attend(n)
+                run(5 + i)
+            if i == QUANT_LAST:
+                quantise_next(3)
+            attend_ready(5 + i, 2)
+        for step in range(16, 20):
+            for work in later.get(step, []):
+                work()
+            attend_ready(step, 4)

@@ -55,6 +55,10 @@ def tile_bottleneck_attention_pa_kernel(tc, qp_top, kp, v, Wv_words, Wv_scales, 
 
         ident = const.tile([P, P], F32)
         make_identity(nc, ident[:])
+        warm_rows = const.tile([P, BANK], BF16)
+        nc.vector.memset(warm_rows[:].bitcast(I32), 0)
+        ones = const.tile([P, P], BF16)
+        nc.vector.memset(ones[:], 1.0)
         warm = const.tile([P, 1], F32)
         nc.vector.memset(warm[:], 0.0)
         nc.scalar.activation(out=warm[:], in_=warm[:], func=ACT.Exp)
@@ -66,8 +70,6 @@ def tile_bottleneck_attention_pa_kernel(tc, qp_top, kp, v, Wv_words, Wv_scales, 
         ident_rows = const.tile([P, P], BF16)
         nc.vector.tensor_copy(out=ident_rows[:], in_=ident[:])
         bias_column = const.tile([P, FEATURE_TILES], F32)
-        ones = const.tile([P, P], BF16)
-        nc.vector.memset(ones[:], 1.0)
         bias = const.tile([P, DV], BF16)
         w_scales = const.tile([P, PASSES, DV], U8, align_bytes=64)
         nc.vector.memset(w_scales[:].bitcast(I32), 0)
@@ -77,6 +79,10 @@ def tile_bottleneck_attention_pa_kernel(tc, qp_top, kp, v, Wv_words, Wv_scales, 
 
         def held_bank(shape):
             return psum.tile(shape, F32, name="held", tag="held", bufs=HELD_BANKS)
+
+        idle_bank = passing_bank([P, BANK])
+        for i in range(4):
+            nc.tensor.matmul(out=idle_bank[:], lhsT=ones[:], rhs=warm_rows[:], start=True, stop=True)
 
         def spread_bias():
             for first in range(0, DV, BANK):
@@ -92,11 +98,14 @@ def tile_bottleneck_attention_pa_kernel(tc, qp_top, kp, v, Wv_words, Wv_scales, 
             )
             nc.scalar.copy(out=bias_column[:], in_=column[:])
 
-        def load_rows(rows, pair_of, name):
+        def load_rows(rows, pair_of, name, singly=False):
             pairs = rows.shape[0] // P // PAIR
             tile = rows_pool.tile([P, pairs * PAIR, D], BF16, name=name, tag="rows%d" % pairs, bufs=ROW_BUFS[pairs])
             for i in range(pairs):
-                nc.sync.dma_start(out=tile[:, PAIR * i : PAIR * (i + 1), :], in_=pair_of(rows, i))
+                tiles = range(PAIR * i, PAIR * (i + 1)) if singly else [slice(PAIR * i, PAIR * (i + 1))]
+                for t in tiles:
+                    part = t if singly else slice(0, PAIR)
+                    nc.sync.dma_start(out=tile[:, t, :], in_=pair_of(rows, i)[:, part - PAIR * i if singly else part, :])
             return tile
 
         def query_pair(rows, i):
@@ -117,7 +126,7 @@ def tile_bottleneck_attention_pa_kernel(tc, qp_top, kp, v, Wv_words, Wv_scales, 
         query_rows = []
         key_rows = []
         for b in range(B):
-            query_rows.append(load_rows(qp_top[b], query_pair, "q_rows%d" % b))
+            query_rows.append(load_rows(qp_top[b], query_pair, "q_rows%d" % b, b == 0))
             key_rows.append(load_rows(kp[b], key_pair, "k_rows%d" % b))
         value_rows = {}
         load_values(SEQUENCE[0])
@@ -136,7 +145,7 @@ def tile_bottleneck_attention_pa_kernel(tc, qp_top, kp, v, Wv_words, Wv_scales, 
         for b in SEQUENCE[1:]:
             load_values(b)
 
-        def turn_pair(rows, first, as_weight, copy):
+        def turn_pair(rows, first, as_weight, copies):
             words = rows[:].bitcast(F32)
             grouped = group_pool.tile([P, PASSES, PAIR * P, PACK], BF16, tag="grouped", bufs=GROUPED_BUFS, align_bytes=64)
             step = 2 if as_weight else 1
@@ -150,7 +159,7 @@ def tile_bottleneck_attention_pa_kernel(tc, qp_top, kp, v, Wv_words, Wv_scales, 
                             words[:, first + t, start : start + step * (P - 1) + 1 : step],
                             ident[:],
                         )
-                copy(
+                copies[t](
                     out=grouped[:].bitcast(F32)[:, :, P * t : P * (t + 1), :],
                     in_=turned[:].rearrange("p g u r -> p g r u"),
                 )
@@ -185,14 +194,15 @@ def tile_bottleneck_attention_pa_kernel(tc, qp_top, kp, v, Wv_words, Wv_scales, 
                     )
             return acc[:].rearrange("p t c -> p c t")
 
+        QCOPY = [(nc.vector.tensor_copy, nc.scalar.copy)] * B
         width = P * PACK
         both = range(Q_TILES)
         score = [keep.tile([P, B, width], F32, name="score%d" % s) for s in both]
         last_scores = []
 
         def turn_queries_and_keys(b):
-            return [turn_pair(query_rows[b], 0, False, nc.vector.tensor_copy)] + [
-                turn_pair(key_rows[b], first, False, nc.scalar.copy) for first in range(0, PACK, PAIR)
+            return [turn_pair(query_rows[b], 0, False, QCOPY[b])] + [
+                turn_pair(key_rows[b], first, False, (nc.scalar.copy, nc.scalar.copy)) for first in range(0, PACK, PAIR)
             ]
 
         def quantise_queries_and_keys(grouped):
@@ -243,12 +253,12 @@ def tile_bottleneck_attention_pa_kernel(tc, qp_top, kp, v, Wv_words, Wv_scales, 
                 nc.scalar.activation(out=x, in_=x, func=ACT.Exp, scale=1.0 / 32.0)
 
         def inverse_of_total():
-            logs = [soft.tile([P, width], F32, name="log%d" % s, tag="log", bufs=2) for s in both]
+            roots = [soft.tile([P, width], F32, name="root%d" % s, tag="root", bufs=2) for s in both]
             for s in both:
-                nc.scalar.activation(out=logs[s][:], in_=total[s][:], func=ACT.Ln)
+                nc.scalar.activation(out=roots[s][:], in_=total[s][:], func=ACT.Abs_reciprocal_sqrt)
             inverse = [soft.tile([P, width], F32, name="inverse%d" % s, tag="inverse", bufs=2) for s in both]
             for s in both:
-                nc.scalar.activation(out=inverse[s][:], in_=logs[s][:], func=ACT.Exp, scale=-1.0)
+                nc.scalar.activation(out=inverse[s][:], in_=roots[s][:], func=ACT.Square)
             return inverse
 
         def weights(b, s, inverse):
@@ -266,7 +276,7 @@ def tile_bottleneck_attention_pa_kernel(tc, qp_top, kp, v, Wv_words, Wv_scales, 
 
         def turn_values(b):
             if is_stationary(b):
-                return [turn_pair(value_rows[b], first, True, nc.scalar.copy) for first in range(0, PACK, PAIR)]
+                return [turn_pair(value_rows[b], first, True, (nc.scalar.copy, nc.scalar.copy)) for first in range(0, PACK, PAIR)]
             words = value_rows[b][:].bitcast(F32)
             grouped = group_pool.tile([P, PASSES, L, PACK], BF16, tag="grouped_moving", bufs=1, align_bytes=64)
             for t in range(PACK):
@@ -338,17 +348,17 @@ def tile_bottleneck_attention_pa_kernel(tc, qp_top, kp, v, Wv_words, Wv_scales, 
                 op=ALU.add,
             )
 
-        def quantise_projection(b, u):
-            features = slice(UNIT * u, UNIT * (u + 1))
+        def quantise_projection(b, u, part=slice(0, UNIT)):
+            features = slice(UNIT * u + part.start, UNIT * u + part.stop)
             nc.vector.quantize_mx(
                 out=vp_codes[b][:, features].bitcast(FP8X4),
                 scales=vp_scales[b][:, features],
-                in_=vp_grouped[b, u][:].rearrange("p n t -> p (n t)"),
+                in_=vp_grouped[b, u][:, part, :].rearrange("p n t -> p (n t)"),
             )
 
-        def attend(b, u):
-            features = slice(UNIT * u, UNIT * (u + 1))
-            acc = held_bank([P, Q_TILES, UNIT])
+        def attend(b, u, part=slice(0, UNIT), copy=nc.scalar.copy):
+            features = slice(UNIT * u + part.start, UNIT * u + part.stop)
+            acc = held_bank([P, Q_TILES, part.stop - part.start])
             for s in both:
                 nc.tensor.matmul_mx(
                     out=acc[:, s, :],
@@ -359,8 +369,8 @@ def tile_bottleneck_attention_pa_kernel(tc, qp_top, kp, v, Wv_words, Wv_scales, 
                     start=True,
                     stop=True,
                 )
-            result = store_pool.tile([P, Q_TILES, UNIT], F32)
-            nc.scalar.copy(out=result[:], in_=acc[:])
+            result = store_pool.tile([P, Q_TILES, part.stop - part.start], F32)
+            copy(out=result[:], in_=acc[:])
             nc.sync.dma_start(out=out[b].rearrange("(p s) n -> p s n", s=Q_TILES)[:, :, features], in_=result[:])
 
         vp_grouped = {}
@@ -415,12 +425,13 @@ def tile_bottleneck_attention_pa_kernel(tc, qp_top, kp, v, Wv_words, Wv_scales, 
             b, u = UNIT_ORDER[step]
             project_unit(b, u, later.get(step, []) + ([extra] if extra else []))
             if is_stationary(b):
-                after(step + 1, lambda: quantise_projection(b, u))
-                ready.append((max(step + 3, 8 + 2 * b), b, u))
+                if step < 15:
+                    after(step + 1, lambda: quantise_projection(b, u))
+                    ready.append((max(step + 2, 8 + 2 * b), b, u))
             else:
                 after(step + 1, lambda: turn_projection(b, u))
                 after(step + 2, lambda: quantise_projection(b, u))
-                ready.append((max(step + 4, 8 + 2 * b), b, u))
+                ready.append((max(step + 3, 8 + 2 * b), b, u))
 
         def attend_ready(step, most):
             for entry in [e for e in ready if e[0] <= step][:most]:
@@ -450,7 +461,9 @@ def tile_bottleneck_attention_pa_kernel(tc, qp_top, kp, v, Wv_words, Wv_scales, 
             if i == QUANT_LAST:
                 quantise_next(3)
             attend_ready(5 + i, 2)
-        for step in range(16, 20):
-            for work in later.get(step, []):
-                work()
-            attend_ready(step, 4)
+        halves = [slice(P * c, P * (c + 1)) for c in range(CHUNKS)]
+        for half in halves:
+            quantise_projection(B - 1, UNITS - 1, half)
+        attend_ready(20, 4)
+        for half, copy in zip(halves, (nc.scalar.copy, nc.vector.tensor_copy)):
+            attend(B - 1, UNITS - 1, half, copy)

@@ -145,12 +145,20 @@ def tile_bottleneck_attention_pa_kernel(tc, qp_top, kp, v, Wv_words, Wv_scales, 
         for b in SEQUENCE[1:]:
             load_values(b)
 
-        def turn_pair(rows, first, as_weight, copies):
+        def turn_pair(rows, first, as_weight, copies, stay_warm=False):
             words = rows[:].bitcast(F32)
             grouped = group_pool.tile([P, PASSES, PAIR * P, PACK], BF16, tag="grouped", bufs=GROUPED_BUFS, align_bytes=64)
             step = 2 if as_weight else 1
             for t in range(PAIR):
                 turned = passing_bank([P, PASSES, 2, P])
+                if stay_warm and t == 0:
+                    nc.tensor.matmul(
+                        out=turned[:].rearrange("p g u r -> p (g u r)"),
+                        lhsT=ones[:],
+                        rhs=warm_rows[:],
+                        start=True,
+                        stop=True,
+                    )
                 for g in range(PASSES):
                     for u in range(2):
                         start = WORDS * g + (u if as_weight else P * u)
@@ -202,7 +210,7 @@ def tile_bottleneck_attention_pa_kernel(tc, qp_top, kp, v, Wv_words, Wv_scales, 
 
         def turn_queries_and_keys(b):
             return [turn_pair(query_rows[b], 0, False, QCOPY[b])] + [
-                turn_pair(key_rows[b], first, False, (nc.scalar.copy, nc.scalar.copy)) for first in range(0, PACK, PAIR)
+                turn_pair(key_rows[b], first, False, (nc.scalar.copy, nc.scalar.copy), True) for first in range(0, PACK, PAIR)
             ]
 
         def quantise_queries_and_keys(grouped):

@@ -128,8 +128,6 @@ def tile_bottleneck_attention_pa_kernel(tc, qp_top, kp, v, Wv_words, Wv_scales, 
         for b in range(B):
             query_rows.append(load_rows(qp_top[b], query_pair, "q_rows%d" % b, b == 0))
             key_rows.append(load_rows(kp[b], key_pair, "k_rows%d" % b))
-        value_rows = {}
-        load_values(SEQUENCE[0])
         nc.sync.dma_start(out=bias_row[0:1, :], in_=bv.unsqueeze(0))
         nc.sync.dma_start(out=bias_rows[0:FEATURE_TILES, :], in_=bv.rearrange("(f p) -> f p", p=P))
         for quadrant in range(4):
@@ -137,6 +135,8 @@ def tile_bottleneck_attention_pa_kernel(tc, qp_top, kp, v, Wv_words, Wv_scales, 
                 out=w_scales[32 * quadrant : 32 * quadrant + 4, :, :].bitcast(I32),
                 in_=Wv_scales[:, 4 * quadrant : 4 * quadrant + 4, :].rearrange("g r n -> r g n").bitcast(I32),
             )
+        value_rows = {}
+        load_values(SEQUENCE[0])
         w_words = const.tile([P, PASSES, DV], U32, align_bytes=64)
         nc.sync.dma_start(
             out=w_words[:].bitcast(I32),

@@ -205,7 +205,10 @@ def tile_bottleneck_attention_pa_kernel(tc, qp_top, kp, v, Wv_words, Wv_scales, 
         QCOPY = [(nc.vector.tensor_copy, nc.scalar.copy)] * B
         width = P * PACK
         both = range(Q_TILES)
-        score = [keep.tile([P, B, width], F32, name="score%d" % s) for s in both]
+        score = keep.tile([P, B, Q_TILES, width], F32, name="score")
+        def as_quad(flat):
+            return flat.rearrange("p (i t) -> p i t", t=PACK)
+
         last_scores = []
 
         def turn_queries_and_keys(b):
@@ -230,53 +233,61 @@ def tile_bottleneck_attention_pa_kernel(tc, qp_top, kp, v, Wv_words, Wv_scales, 
                 if b == B - 1:
                     last_scores.append(quad)
                 else:
-                    nc.scalar.copy(out=score[s][:, b, :].rearrange("p (i t) -> p i t", t=PACK), in_=quad)
+                    nc.scalar.copy(out=as_quad(score[:, b, s, :]), in_=quad)
 
-        top = [soft.tile([P, width], F32, name="top%d" % s, tag="single", bufs=4) for s in both]
-        total = [soft.tile([P, width], F32, name="total%d" % s, tag="single", bufs=4) for s in both]
-        attn_codes = [keep.tile([P, B, P], U32, name="attn_codes%d" % s, align_bytes=64) for s in both]
-        attn_scales = [keep.tile([P, B, P], U8, name="attn_scales%d" % s, align_bytes=64) for s in both]
+        top = soft.tile([P, Q_TILES, width], F32, name="top", bufs=1)
+        total = soft.tile([P, Q_TILES, width], F32, name="total", bufs=1)
+        attn_codes = keep.tile([P, B, Q_TILES, P], U32, name="attn_codes", align_bytes=64)
+        attn_scales = keep.tile([P, B, Q_TILES, P], U8, name="attn_scales", align_bytes=64)
 
-        def as_quad(flat):
-            return flat.rearrange("p (i t) -> p i t", t=PACK)
-
-        def fold(folded, b, op):
+        def raise_top(b):
             for s in both:
-                so_far = score[s][:, 0, :] if b == 1 else folded[s][:]
-                nc.vector.tensor_tensor(out=folded[s][:], in0=so_far, in1=score[s][:, b, :], op=op)
+                so_far = score[:, 0, s] if b == 1 else top[:, s]
+                nc.vector.tensor_tensor(out=top[:, s], in0=so_far, in1=score[:, b, s], op=ALU.max)
 
-        def fold_top_of_last():
+        def raise_top_by_last():
             for s in both:
-                nc.vector.tensor_tensor(out=as_quad(top[s][:]), in0=last_scores[s], in1=as_quad(top[s][:]), op=ALU.max)
+                nc.vector.tensor_tensor(
+                    out=as_quad(top[:, s]), in0=last_scores[s], in1=as_quad(top[:, s]), op=ALU.max
+                )
+
+        def add_up():
+            for b in range(1, B):
+                for s in both:
+                    so_far = score[:, 0, s] if b == 1 else total[:, s]
+                    nc.vector.tensor_tensor(out=total[:, s], in0=so_far, in1=score[:, b, s], op=ALU.add)
 
         def shift_and_exp(b):
             for s in both:
-                x = score[s][:, b, :]
-                if b == B - 1:
-                    nc.vector.tensor_tensor(
-                        out=as_quad(x), in0=last_scores[s], in1=as_quad(top[s][:]), op=ALU.subtract
-                    )
-                else:
-                    nc.vector.tensor_tensor(out=x, in0=x, in1=top[s][:], op=ALU.subtract)
+                x = score[:, b, s]
+                nc.vector.tensor_tensor(out=x, in0=x, in1=top[:, s], op=ALU.subtract)
+                nc.scalar.activation(out=x, in_=x, func=ACT.Exp, scale=1.0 / 32.0)
+
+        def shift_and_exp_last():
+            for s in both:
+                x = score[:, B - 1, s]
+                nc.vector.tensor_tensor(out=as_quad(x), in0=last_scores[s], in1=as_quad(top[:, s]), op=ALU.subtract)
                 nc.scalar.activation(out=x, in_=x, func=ACT.Exp, scale=1.0 / 32.0)
 
         def inverse_of_total():
-            roots = [soft.tile([P, width], F32, name="root%d" % s, tag="root", bufs=2) for s in both]
+            inverse = soft.tile([P, Q_TILES, width], F32, name="inverse", bufs=1)
+            root = soft.tile([P, Q_TILES, width], F32, name="root", bufs=1)
             for s in both:
-                nc.scalar.activation(out=roots[s][:], in_=total[s][:], func=ACT.Abs_reciprocal_sqrt)
-            inverse = [soft.tile([P, width], F32, name="inverse%d" % s, tag="inverse", bufs=2) for s in both]
+                nc.scalar.activation(out=root[:, s], in_=total[:, s], func=ACT.Abs_reciprocal_sqrt)
             for s in both:
-                nc.scalar.activation(out=inverse[s][:], in_=roots[s][:], func=ACT.Square)
+                nc.scalar.activation(out=inverse[:, s], in_=root[:, s], func=ACT.Square)
             return inverse
 
-        def weights(b, s, inverse):
-            attn = soft.tile([P, width], BF16, name="attn", tag="attn", bufs=2, align_bytes=64)
-            nc.vector.tensor_tensor(out=attn[:], in0=score[s][:, b, :], in1=inverse[s][:], op=ALU.mult)
+        def weights(b, inverse):
+            attn = soft.tile([P, Q_TILES, width], BF16, name="attn", tag="attn", bufs=2, align_bytes=64)
+            nc.vector.tensor_tensor(out=attn[:], in0=score[:, b], in1=inverse[:], op=ALU.mult)
             return attn
 
-        def quantise_weights(b, s, attn):
+        def quantise_weights(b, attn):
             nc.vector.quantize_mx(
-                out=attn_codes[s][:, b, :].bitcast(FP8X4), scales=attn_scales[s][:, b, :], in_=attn[:]
+                out=attn_codes[:, b].rearrange("p s i -> p (s i)").bitcast(FP8X4),
+                scales=attn_scales[:, b].rearrange("p s i -> p (s i)"),
+                in_=attn[:].rearrange("p s c -> p (s c)"),
             )
 
         vp_codes = [keep.tile([P, DV], U32, name="vp_codes%d" % b, align_bytes=64) for b in range(B)]
@@ -342,7 +353,7 @@ def tile_bottleneck_attention_pa_kernel(tc, qp_top, kp, v, Wv_words, Wv_scales, 
                 for h in range(2):
                     nc.tensor.transpose(bank[:, c, h, :], words[:, c, P * h : P * (h + 1)], ident[:])
             (nc.vector.tensor_copy if (b, u) in WORDS_ON_VECTOR else nc.scalar.copy)(
-                out=vp_grouped[b, u][:].bitcast(F32).rearrange("p (c n) h -> p c n h", c=CHUNKS),
+                out=vp_grouped[b, u].bitcast(F32).rearrange("p (c n) h -> p c n h", c=CHUNKS),
                 in_=bank[:].rearrange("p c h n -> p c n h"),
             )
 
@@ -356,12 +367,12 @@ def tile_bottleneck_attention_pa_kernel(tc, qp_top, kp, v, Wv_words, Wv_scales, 
                 op=ALU.add,
             )
 
-        def quantise_projection(b, u, part=slice(0, UNIT)):
-            features = slice(UNIT * u + part.start, UNIT * u + part.stop)
+        def quantise_projection(b, grouped, first):
+            features = slice(first, first + grouped.shape[1])
             nc.vector.quantize_mx(
                 out=vp_codes[b][:, features].bitcast(FP8X4),
                 scales=vp_scales[b][:, features],
-                in_=vp_grouped[b, u][:, part, :].rearrange("p n t -> p (n t)"),
+                in_=grouped.rearrange("p n t -> p (n t)"),
             )
 
         def attend(b, u, part=slice(0, UNIT), copy=nc.scalar.copy):
@@ -370,8 +381,8 @@ def tile_bottleneck_attention_pa_kernel(tc, qp_top, kp, v, Wv_words, Wv_scales, 
             for s in both:
                 nc.tensor.matmul_mx(
                     out=acc[:, s, :],
-                    lhsT=attn_codes[s][:, b, :].bitcast(FP8X4),
-                    lhsT_scale=attn_scales[s][:, b, :],
+                    lhsT=attn_codes[:, b, s, :].bitcast(FP8X4),
+                    lhsT_scale=attn_scales[:, b, s, :],
                     rhs=vp_codes[b][:, features].bitcast(FP8X4),
                     rhs_scale=vp_scales[b][:, features],
                     start=True,
@@ -382,10 +393,15 @@ def tile_bottleneck_attention_pa_kernel(tc, qp_top, kp, v, Wv_words, Wv_scales, 
             nc.sync.dma_start(out=out[b].rearrange("(p s) n -> p s n", s=Q_TILES)[:, :, features], in_=result[:])
 
         vp_grouped = {}
+        vp_pair = {}
         turned_vp = {}
 
         def project_unit(b, u, between):
-            vp_grouped[b, u] = group_pool.tile([P, UNIT, PACK], BF16, name="vp_grouped%d_%d" % (b, u), tag="vp_grouped", bufs=4, align_bytes=64)
+            if u % 2 == 0:
+                pair = group_pool.tile([P, 2 * UNIT, PACK], BF16, name="vp_grouped%d_%d" % (b, u), tag="vp_grouped", bufs=3, align_bytes=64)
+                for half in range(2):
+                    vp_grouped[b, u + half] = pair[:, UNIT * half : UNIT * (half + 1), :]
+                vp_pair[b, u] = pair[:]
             if not is_stationary(b):
                 turned_vp[b, u] = group_pool.tile([P, CHUNKS, L], BF16, name="turned_vp%d_%d" % (b, u), tag="turned_vp", bufs=3, align_bytes=64)
             for c in range(CHUNKS):
@@ -414,10 +430,10 @@ def tile_bottleneck_attention_pa_kernel(tc, qp_top, kp, v, Wv_words, Wv_scales, 
                 grouped = turn_queries_and_keys(b + 1)
             scores(b, q_mx, k_mx)
             if b >= 2:
-                fold(top, b - 1, ALU.max)
+                raise_top(b - 1)
         turn_next(0)
-        fold_top_of_last()
-        shift_and_exp(3)
+        raise_top_by_last()
+        shift_and_exp_last()
         quantise_next(0)
         spread_bias()
         for b in (0, 1, 2):
@@ -433,12 +449,17 @@ def tile_bottleneck_attention_pa_kernel(tc, qp_top, kp, v, Wv_words, Wv_scales, 
             b, u = UNIT_ORDER[step]
             project_unit(b, u, later.get(step, []) + ([extra] if extra else []))
             if is_stationary(b):
-                if step < 15:
-                    after(step + 1, lambda: quantise_projection(b, u))
-                    ready.append((max(step + 2, 8 + 2 * b), b, u))
+                if b >= 2:
+                    if (b, u) != UNIT_ORDER[-1]:
+                        after(step + 1, lambda: quantise_projection(b, vp_grouped[b, u], UNIT * u))
+                        ready.append((max(step + 2, 8 + 2 * b), b, u))
+                elif u % 2 == 1:
+                    after(step + 1, lambda: quantise_projection(b, vp_pair[b, u - 1], UNIT * (u - 1)))
+                    for v_ in (u - 1, u):
+                        ready.append((max(step + 2, 8 + 2 * b), b, v_))
             else:
                 after(step + 1, lambda: turn_projection(b, u))
-                after(step + 2, lambda: quantise_projection(b, u))
+                after(step + 2, lambda: quantise_projection(b, vp_grouped[b, u], UNIT * u))
                 ready.append((max(step + 3, 8 + 2 * b), b, u))
 
         def attend_ready(step, most):
@@ -448,8 +469,7 @@ def tile_bottleneck_attention_pa_kernel(tc, qp_top, kp, v, Wv_words, Wv_scales, 
 
         run(0)
         turn_next(1)
-        for b in range(1, B):
-            fold(total, b, ALU.add)
+        add_up()
         run(1)
         run(2)
         quantise_next(1)
@@ -460,18 +480,16 @@ def tile_bottleneck_attention_pa_kernel(tc, qp_top, kp, v, Wv_words, Wv_scales, 
         quantise_next(2)
         turn_next(3)
         for i in range(11):
-            if i < 2 * B:
-                b, s = divmod(i, 2)
-                attn = weights(b, s, inverse)
-                run(5 + i, lambda: quantise_weights(b, s, attn))
-            else:
-                run(5 + i)
+            b = i // 2
+            if i % 2 == 0 and b < B:
+                attn = weights(b, inverse)
+            run(5 + i, (lambda: quantise_weights(b, attn)) if i % 2 == 1 and b < B else None)
             if i == QUANT_LAST:
                 quantise_next(3)
             attend_ready(5 + i, 2)
         halves = [slice(P * c, P * (c + 1)) for c in range(CHUNKS)]
         for half in halves:
-            quantise_projection(B - 1, UNITS - 1, half)
+            quantise_projection(B - 1, vp_grouped[B - 1, UNITS - 1][:, half, :], UNIT * (UNITS - 1) + half.start)
         attend_ready(20, 4)
         for half, copy in zip(halves, (nc.scalar.copy, nc.vector.tensor_copy)):
             attend(B - 1, UNITS - 1, half, copy)

from contextlib import ExitStack

import concourse.mybir as mybir
from concourse.masks import make_identity

BF16 = mybir.dt.bfloat16
F32 = mybir.dt.float32
I32 = mybir.dt.int32
U32 = mybir.dt.uint32
U8 = mybir.dt.uint8
FP8X4 = mybir.dt.float8_e4m3fn_x4
ACT = mybir.ActivationFunctionType
ALU = mybir.AluOpType

B, L, D, DV, BN = 4, 512, 1024, 1024, 256
P = 128
PACK = 4
K_PASS = P * PACK
PASSES = D // K_PASS
WORDS = K_PASS // 2
PAIR = 2
Q_TILES = BN // P
BANK = 512
UNIT = BANK // Q_TILES
UNITS = DV // UNIT
CHUNKS = UNIT // P
PASSING_BANKS = 6
HELD_BANKS = 2
GROUPED_BUFS = 6

ROW_BUFS = (0, 4, 6)
FEATURE_TILES = DV // P
STATIONARY = (0, 1, 3)
SEQUENCE = (0, 1, 2, 3)
UNIT_ORDER = [(0, 0), (0, 1), (0, 2), (0, 3), (1, 0), (1, 1), (1, 2), (1, 3), (2, 0), (2, 1), (2, 2), (2, 3), (3, 0), (3, 1), (3, 2), (3, 3)]
TURN_LAST = 0
QUANT_LAST = 3
BIAS_ON_VECTOR = ()
WORDS_ON_VECTOR = ()

FLOPS = 2 * B * (L * D * DV + BN * L * D + BN * L * DV)


def tile_bottleneck_attention_pa_kernel(tc, qp_top, kp, v, Wv_words, Wv_scales, bv, out):
    nc = tc.nc
    with ExitStack() as ctx:
        const = ctx.enter_context(tc.tile_pool(name="const", bufs=1))
        rows_pool = ctx.enter_context(tc.tile_pool(name="rows", bufs=1))
        group_pool = ctx.enter_context(tc.tile_pool(name="group", bufs=2))
        code_pool = ctx.enter_context(tc.tile_pool(name="code", bufs=2))
        keep = ctx.enter_context(tc.tile_pool(name="keep", bufs=1))
        soft = ctx.enter_context(tc.tile_pool(name="soft", bufs=2))
        store_pool = ctx.enter_context(tc.tile_pool(name="store", bufs=6))
        psum = ctx.enter_context(tc.psum_pool(name="psum", bufs=1))

        ident = const.tile([P, P], F32)
        make_identity(nc, ident[:])
        warm_rows = const.tile([P, BANK], BF16)
        nc.vector.memset(warm_rows[:].bitcast(I32), 0)
        ones = const.tile([P, P], BF16)
        nc.vector.memset(ones[:], 1.0)
        warm = const.tile([P, 1], F32)
        nc.vector.memset(warm[:], 0.0)
        nc.scalar.activation(out=warm[:], in_=warm[:], func=ACT.Exp)

        bias_row = const.tile([P, DV], BF16)
        nc.vector.memset(bias_row[:].bitcast(I32), 0)
        bias_rows = const.tile([P, P], BF16)
        nc.vector.memset(bias_rows[:].bitcast(I32), 0)
        ident_rows = const.tile([P, P], BF16)
        nc.vector.tensor_copy(out=ident_rows[:], in_=ident[:])
        bias_column = const.tile([P, FEATURE_TILES], F32)
        bias = const.tile([P, DV], BF16)
        w_scales = const.tile([P, PASSES, DV], U8, align_bytes=64)
        nc.vector.memset(w_scales[:].bitcast(I32), 0)

        def passing_bank(shape):
            return psum.tile(shape, F32, name="passing", tag="passing", bufs=PASSING_BANKS)

        def held_bank(shape):
            return psum.tile(shape, F32, name="held", tag="held", bufs=HELD_BANKS)

        idle_bank = passing_bank([P, BANK])
        for i in range(4):
            nc.tensor.matmul(out=idle_bank[:], lhsT=ones[:], rhs=warm_rows[:], start=True, stop=True)

        def spread_bias():
            for first in range(0, DV, BANK):
                spread = passing_bank([P, BANK])
                nc.tensor.matmul(
                    out=spread[:], lhsT=ones[:], rhs=bias_row[:, first : first + BANK], start=True, stop=True
                )
                nc.scalar.copy(out=bias[:, first : first + BANK], in_=spread[:])

            column = passing_bank([P, FEATURE_TILES])
            nc.tensor.matmul(
                out=column[:], lhsT=bias_rows[:], rhs=ident_rows[:, 0:FEATURE_TILES], start=True, stop=True
            )
            nc.scalar.copy(out=bias_column[:], in_=column[:])

        def load_rows(rows, pair_of, name, singly=False):
            pairs = rows.shape[0] // P // PAIR
            tile = rows_pool.tile([P, pairs * PAIR, D], BF16, name=name, tag="rows%d" % pairs, bufs=ROW_BUFS[pairs])
            for i in range(pairs):
                tiles = range(PAIR * i, PAIR * (i + 1)) if singly else [slice(PAIR * i, PAIR * (i + 1))]
                for t in tiles:
                    part = t if singly else slice(0, PAIR)
                    nc.sync.dma_start(out=tile[:, t, :], in_=pair_of(rows, i)[:, part - PAIR * i if singly else part, :])
            return tile

        def query_pair(rows, i):
            return rows.rearrange("(p s) d -> p s d", s=Q_TILES)

        def key_pair(rows, i):
            return rows.rearrange("(u p e) d -> u p e d", p=P, e=PAIR)[i]

        def plain_pair(rows, i):
            return rows.rearrange("(t p) d -> p t d", p=P)[:, PAIR * i : PAIR * (i + 1), :]

        def is_stationary(b):
            return b in STATIONARY

        def load_values(b):
            value_rows[b] = load_rows(v[b], key_pair if is_stationary(b) else plain_pair, "v_rows%d" % b)

        query_rows = []
        key_rows = []
        for b in range(B):
            query_rows.append(load_rows(qp_top[b], query_pair, "q_rows%d" % b, b == 0))
            key_rows.append(load_rows(kp[b], key_pair, "k_rows%d" % b))
        nc.sync.dma_start(out=bias_row[0:1, :], in_=bv.unsqueeze(0))
        nc.sync.dma_start(out=bias_rows[0:FEATURE_TILES, :], in_=bv.rearrange("(f p) -> f p", p=P))
        for quadrant in range(4):
            nc.sync.dma_start(
                out=w_scales[32 * quadrant : 32 * quadrant + 4, :, :].bitcast(I32),
                in_=Wv_scales[:, 4 * quadrant : 4 * quadrant + 4, :].rearrange("g r n -> r g n").bitcast(I32),
            )
        value_rows = {}
        load_values(SEQUENCE[0])
        w_words = const.tile([P, PASSES, DV], U32, align_bytes=64)
        nc.sync.dma_start(
            out=w_words[:].bitcast(I32),
            in_=Wv_words.rearrange("g p n t -> p g (n t)").bitcast(I32),
        )
        for b in SEQUENCE[1:]:
            load_values(b)

        def turn_pair(rows, first, as_weight, copies, stay_warm=False):
            words = rows[:].bitcast(F32)
            grouped = group_pool.tile([P, PASSES, PAIR * P, PACK], BF16, tag="grouped", bufs=GROUPED_BUFS, align_bytes=64)
            step = 2 if as_weight else 1
            for t in range(PAIR):
                turned = passing_bank([P, PASSES, 2, P])
                if stay_warm and t == 0:
                    nc.tensor.matmul(
                        out=turned[:].rearrange("p g u r -> p (g u r)"),
                        lhsT=ones[:],
                        rhs=warm_rows[:],
                        start=True,
                        stop=True,
                    )
                for g in range(PASSES):
                    for u in range(2):
                        start = WORDS * g + (u if as_weight else P * u)
                        nc.tensor.transpose(
                            turned[:, g, u, :],
                            words[:, first + t, start : start + step * (P - 1) + 1 : step],
                            ident[:],
                        )
                copies[t](
                    out=grouped[:].bitcast(F32)[:, :, P * t : P * (t + 1), :],
                    in_=turned[:].rearrange("p g u r -> p g r u"),
                )
            return grouped

        def quantise_pair(grouped, codes, scales):
            nc.vector.quantize_mx(
                out=codes.rearrange("p g c -> p (g c)").bitcast(FP8X4),
                scales=scales.rearrange("p g c -> p (g c)"),
                in_=grouped[:].rearrange("p g c f -> p (g c f)"),
            )

        def new_codes(pairs, tag):
            codes = code_pool.tile([P, pairs, PASSES, PAIR * P], U32, tag=tag + "_codes", align_bytes=64)
            scales = code_pool.tile([P, pairs, PASSES, PAIR * P], U8, tag=tag + "_scales", align_bytes=64)
            return codes, scales

        def multiply_quad(keys_mx, moving_of_pass, new_bank):
            acc = new_bank([P, PACK, P])
            for t in range(PACK):
                rows = slice(P * (t % PAIR), P * (t % PAIR + 1))
                for g in range(PASSES):
                    moving = moving_of_pass(g)
                    nc.tensor.matmul_mx(
                        out=acc[:, t, :],
                        lhsT=keys_mx[0][:, t // PAIR, g, rows].bitcast(FP8X4),
                        lhsT_scale=keys_mx[1][:, t // PAIR, g, rows],
                        rhs=moving[0].bitcast(FP8X4),
                        rhs_scale=moving[1],
                        start=(g == 0),
                        stop=(g == PASSES - 1),
                    )
            return acc[:].rearrange("p t c -> p c t")

        QCOPY = [(nc.vector.tensor_copy, nc.scalar.copy)] * B
        width = P * PACK
        both = range(Q_TILES)
        score = keep.tile([P, B, Q_TILES, width], F32, name="score")
        def as_quad(flat):
            return flat.rearrange("p (i t) -> p i t", t=PACK)

        last_scores = []

        def turn_queries_and_keys(b):
            return [turn_pair(query_rows[b], 0, False, QCOPY[b])] + [
                turn_pair(key_rows[b], first, False, (nc.scalar.copy, nc.scalar.copy), True) for first in range(0, PACK, PAIR)
            ]

        def quantise_queries_and_keys(grouped):
            q_mx = new_codes(1, "q")
            k_mx = new_codes(PACK // PAIR, "k")
            quantise_pair(grouped[1], k_mx[0][:, 0], k_mx[1][:, 0])
            quantise_pair(grouped[0], q_mx[0][:, 0], q_mx[1][:, 0])
            quantise_pair(grouped[2], k_mx[0][:, 1], k_mx[1][:, 1])
            return q_mx, k_mx

        def scores(b, q_mx, k_mx):
            for s in both:
                queries = slice(P * s, P * (s + 1))
                quad = multiply_quad(
                    k_mx, lambda g: (q_mx[0][:, 0, g, queries], q_mx[1][:, 0, g, queries]), held_bank
                )
                if b == B - 1:
                    last_scores.append(quad)
                else:
                    nc.scalar.copy(out=as_quad(score[:, b, s, :]), in_=quad)

        top = soft.tile([P, Q_TILES, width], F32, name="top", bufs=1)
        total = soft.tile([P, Q_TILES, width], F32, name="total", bufs=1)
        attn_codes = keep.tile([P, B, Q_TILES, P], U32, name="attn_codes", align_bytes=64)
        attn_scales = keep.tile([P, B, Q_TILES, P], U8, name="attn_scales", align_bytes=64)

        def raise_top(b):
            for s in both:
                so_far = score[:, 0, s] if b == 1 else top[:, s]
                nc.vector.tensor_tensor(out=top[:, s], in0=so_far, in1=score[:, b, s], op=ALU.max)

        def raise_top_by_last():
            for s in both:
                nc.vector.tensor_tensor(
                    out=as_quad(top[:, s]), in0=last_scores[s], in1=as_quad(top[:, s]), op=ALU.max
                )

        def add_up():
            for b in range(1, B):
                for s in both:
                    so_far = score[:, 0, s] if b == 1 else total[:, s]
                    nc.vector.tensor_tensor(out=total[:, s], in0=so_far, in1=score[:, b, s], op=ALU.add)

        def shift_and_exp(b):
            for s in both:
                x = score[:, b, s]
                nc.vector.tensor_tensor(out=x, in0=x, in1=top[:, s], op=ALU.subtract)
                nc.scalar.activation(out=x, in_=x, func=ACT.Exp, scale=1.0 / 32.0)

        def shift_and_exp_last():
            for s in both:
                x = score[:, B - 1, s]
                nc.vector.tensor_tensor(out=as_quad(x), in0=last_scores[s], in1=as_quad(top[:, s]), op=ALU.subtract)
                nc.scalar.activation(out=x, in_=x, func=ACT.Exp, scale=1.0 / 32.0)

        def inverse_of_total():
            inverse = soft.tile([P, Q_TILES, width], F32, name="inverse", bufs=1)
            root = soft.tile([P, Q_TILES, width], F32, name="root", bufs=1)
            for s in both:
                nc.scalar.activation(out=root[:, s], in_=total[:, s], func=ACT.Abs_reciprocal_sqrt)
            for s in both:
                nc.scalar.activation(out=inverse[:, s], in_=root[:, s], func=ACT.Square)
            return inverse

        def weights(b, inverse):
            attn = soft.tile([P, Q_TILES, width], BF16, name="attn", tag="attn", bufs=2, align_bytes=64)
            nc.vector.tensor_tensor(out=attn[:], in0=score[:, b], in1=inverse[:], op=ALU.mult)
            return attn

        def quantise_weights(b, attn):
            nc.vector.quantize_mx(
                out=attn_codes[:, b].rearrange("p s i -> p (s i)").bitcast(FP8X4),
                scales=attn_scales[:, b].rearrange("p s i -> p (s i)"),
                in_=attn[:].rearrange("p s c -> p (s c)"),
            )

        vp_codes = [keep.tile([P, DV], U32, name="vp_codes%d" % b, align_bytes=64) for b in range(B)]
        vp_scales = [keep.tile([P, DV], U8, name="vp_scales%d" % b, align_bytes=64) for b in range(B)]

        def turn_values(b):
            if is_stationary(b):
                return [turn_pair(value_rows[b], first, True, (nc.scalar.copy, nc.scalar.copy)) for first in range(0, PACK, PAIR)]
            words = value_rows[b][:].bitcast(F32)
            grouped = group_pool.tile([P, PASSES, L, PACK], BF16, tag="grouped_moving", bufs=1, align_bytes=64)
            for t in range(PACK):
                turned = passing_bank([P, PASSES, 2, P])
                for g in range(PASSES):
                    for u in range(2):
                        start = WORDS * g + u
                        nc.tensor.transpose(
                            turned[:, g, u, :], words[:, t, start : start + 2 * (P - 1) + 1 : 2], ident[:]
                        )
                nc.scalar.copy(
                    out=grouped[:].bitcast(F32)[:, :, P * t : P * (t + 1), :],
                    in_=turned[:].rearrange("p g u r -> p g r u"),
                )
            return grouped

        def quantise_values(b, grouped):
            v_mx = new_codes(PACK // PAIR, "v")
            if is_stationary(b):
                for pair in range(PACK // PAIR):
                    quantise_pair(grouped[pair], v_mx[0][:, pair], v_mx[1][:, pair])
                return v_mx
            codes = v_mx[0][:].rearrange("p a g c -> p (a g c)").rearrange("p (g c) -> p g c", g=PASSES)
            scales = v_mx[1][:].rearrange("p a g c -> p (a g c)").rearrange("p (g c) -> p g c", g=PASSES)
            for g in range(PASSES):
                nc.vector.quantize_mx(
                    out=codes[:, g].bitcast(FP8X4),
                    scales=scales[:, g],
                    in_=grouped[:, g].rearrange("p c f -> p (c f)"),
                )
            return codes, scales

        def project_tile(b, f, codes, scales, turned_vp, half):
            features = slice(P * f, P * (f + 1))
            acc = passing_bank([P, L])
            for g in range(PASSES):
                nc.tensor.matmul_mx(
                    out=acc[:],
                    lhsT=w_words[:, g, features].bitcast(FP8X4),
                    lhsT_scale=w_scales[:, g, features],
                    rhs=codes[:, g].bitcast(FP8X4),
                    rhs_scale=scales[:, g],
                    start=(g == 0),
                    stop=(g == PASSES - 1),
                )
            if (b, f) in BIAS_ON_VECTOR:
                nc.vector.tensor_scalar(out=turned_vp[:, half, :], in0=acc[:], scalar1=bias_column[:, f : f + 1], scalar2=None, op0=ALU.add)
            else:
                nc.scalar.activation(out=turned_vp[:, half, :], in_=acc[:], func=ACT.Identity, bias=bias_column[:, f : f + 1])

        def turn_projection(b, u):
            words = turned_vp[b, u][:].bitcast(F32)
            bank = passing_bank([P, CHUNKS, 2, P])
            for c in range(CHUNKS):
                for h in range(2):
                    nc.tensor.transpose(bank[:, c, h, :], words[:, c, P * h : P * (h + 1)], ident[:])
            (nc.vector.tensor_copy if (b, u) in WORDS_ON_VECTOR else nc.scalar.copy)(
                out=vp_grouped[b, u].bitcast(F32).rearrange("p (c n) h -> p c n h", c=CHUNKS),
                in_=bank[:].rearrange("p c h n -> p c n h"),
            )

        def project_chunk(u, c, v_mx, vp_grouped):
            features = slice(UNIT * u + P * c, UNIT * u + P * (c + 1))
            quad = multiply_quad(v_mx, lambda g: (w_words[:, g, features], w_scales[:, g, features]), passing_bank)
            nc.vector.tensor_tensor(
                out=vp_grouped[:, P * c : P * (c + 1), :],
                in0=quad,
                in1=bias[:, features].unsqueeze(2).to_broadcast([P, P, PACK]),
                op=ALU.add,
            )

        def quantise_projection(b, grouped, first):
            features = slice(first, first + grouped.shape[1])
            nc.vector.quantize_mx(
                out=vp_codes[b][:, features].bitcast(FP8X4),
                scales=vp_scales[b][:, features],
                in_=grouped.rearrange("p n t -> p (n t)"),
            )

        def attend(b, u, part=slice(0, UNIT), copy=nc.scalar.copy):
            features = slice(UNIT * u + part.start, UNIT * u + part.stop)
            acc = held_bank([P, Q_TILES, part.stop - part.start])
            for s in both:
                nc.tensor.matmul_mx(
                    out=acc[:, s, :],
                    lhsT=attn_codes[:, b, s, :].bitcast(FP8X4),
                    lhsT_scale=attn_scales[:, b, s, :],
                    rhs=vp_codes[b][:, features].bitcast(FP8X4),
                    rhs_scale=vp_scales[b][:, features],
                    start=True,
                    stop=True,
                )
            result = store_pool.tile([P, Q_TILES, part.stop - part.start], F32)
            copy(out=result[:], in_=acc[:])
            nc.sync.dma_start(out=out[b].rearrange("(p s) n -> p s n", s=Q_TILES)[:, :, features], in_=result[:])

        vp_grouped = {}
        vp_pair = {}
        turned_vp = {}

        def project_unit(b, u, between):
            if u % 2 == 0:
                pair = group_pool.tile([P, 2 * UNIT, PACK], BF16, name="vp_grouped%d_%d" % (b, u), tag="vp_grouped", bufs=3, align_bytes=64)
                for half in range(2):
                    vp_grouped[b, u + half] = pair[:, UNIT * half : UNIT * (half + 1), :]
                vp_pair[b, u] = pair[:]
            if not is_stationary(b):
                turned_vp[b, u] = group_pool.tile([P, CHUNKS, L], BF16, name="turned_vp%d_%d" % (b, u), tag="turned_vp", bufs=3, align_bytes=64)
            for c in range(CHUNKS):
                if is_stationary(b):
                    project_chunk(u, c, v_mx[b], vp_grouped[b, u])
                else:
                    project_tile(b, CHUNKS * u + c, v_mx[b][0], v_mx[b][1], turned_vp[b, u], c)
                if c == 0:
                    for work in between:
                        work()

        v_mx = {}
        v_grouped = {}

        def turn_next(i):
            v_grouped[SEQUENCE[i]] = turn_values(SEQUENCE[i])

        def quantise_next(i):
            b = SEQUENCE[i]
            v_mx[b] = quantise_values(b, v_grouped[b])

        grouped = turn_queries_and_keys(0)
        for b in range(B):
            q_mx, k_mx = quantise_queries_and_keys(grouped)
            if b + 1 < B:
                grouped = turn_queries_and_keys(b + 1)
            scores(b, q_mx, k_mx)
            if b >= 2:
                raise_top(b - 1)
        turn_next(0)
        raise_top_by_last()
        shift_and_exp_last()
        quantise_next(0)
        spread_bias()
        for b in (0, 1, 2):
            shift_and_exp(b)

        later = {}
        ready = []

        def after(step, work):
            later.setdefault(step, []).append(work)

        def run(step, extra=None):
            b, u = UNIT_ORDER[step]
            project_unit(b, u, later.get(step, []) + ([extra] if extra else []))
            if is_stationary(b):
                if b >= 2:
                    if (b, u) != UNIT_ORDER[-1]:
                        after(step + 1, lambda: quantise_projection(b, vp_grouped[b, u], UNIT * u))
                        ready.append((max(step + 2, 8 + 2 * b), b, u))
                elif u % 2 == 1:
                    after(step + 1, lambda: quantise_projection(b, vp_pair[b, u - 1], UNIT * (u - 1)))
                    for v_ in (u - 1, u):
                        ready.append((max(step + 2, 8 + 2 * b), b, v_))
            else:
                after(step + 1, lambda: turn_projection(b, u))
                after(step + 2, lambda: quantise_projection(b, vp_grouped[b, u], UNIT * u))
                ready.append((max(step + 3, 8 + 2 * b), b, u))

        def attend_ready(step, most):
            for entry in [e for e in ready if e[0] <= step][:most]:
                attend(entry[1], entry[2])
                ready.remove(entry)

        run(0)
        turn_next(1)
        add_up()
        run(1)
        run(2)
        quantise_next(1)
        turn_next(2)
        inverse = inverse_of_total()
        run(3)
        run(4)
        quantise_next(2)
        turn_next(3)
        for i in range(11):
            b = i // 2
            if i % 2 == 0 and b < B:
                attn = weights(b, inverse)
            run(5 + i, (lambda: quantise_weights(b, attn)) if i % 2 == 1 and b < B else None)
            if i == QUANT_LAST:
                quantise_next(3)
            attend_ready(5 + i, 2)
        halves = [slice(P * c, P * (c + 1)) for c in range(CHUNKS)]
        for half in halves:
            quantise_projection(B - 1, vp_grouped[B - 1, UNITS - 1][:, half, :], UNIT * (UNITS - 1) + half.start)
        attend_ready(20, 4)
        for half, copy in zip(halves, (nc.scalar.copy, nc.vector.tensor_copy)):
            attend(B - 1, UNITS - 1, half, copy)
